import numpy as np
import ml_dtypes


def mxq(x, axis, fmt="e4m3"):
    dtype, down = {"e4m3": (ml_dtypes.float8_e4m3fn, 7), "e5m2": (ml_dtypes.float8_e5m2, 14)}[fmt]
    v = np.moveaxis(np.asarray(x, np.float32).astype(ml_dtypes.bfloat16).astype(np.float64), axis, -1)
    blocks = v.reshape(v.shape[:-1] + (-1, 32))
    amax = np.abs(blocks).max(-1, keepdims=True)
    byte = np.maximum(np.where(amax > 0, np.frexp(amax)[1] - 1 + 127, 0) - down, 1)
    scale = np.exp2(byte - 127.0)
    codes = (blocks / scale).astype(np.float32).astype(dtype).astype(np.float64)
    return np.moveaxis((codes * scale).reshape(v.shape), -1, axis)


WIDE = False


def mx_kscale(k):
    if not WIDE:
        return np.ones(k)
    levels = np.array([10, -10, 5, -5, 0])
    a = np.random.permutation(np.resize(levels, k // 512 * 4)).reshape(k // 512, 4)
    idx = np.arange(k)
    return np.exp2(a[idx // 512, idx % 128 // 32])


BF16 = ml_dtypes.bfloat16


def bf(x):
    return np.asarray(x, np.float32).astype(BF16)


def f64(x):
    return np.asarray(x).astype(np.float64)


B, S, DIM, H, NOPE, ROPE_SP, V_SP, KV_RANK = 2, 256, 2048, 16, 64, 128, 128, 512
C = 1.0
EPS = 1e-6


def lift(sp):
    return np.concatenate([np.sqrt((sp * sp).sum(-1, keepdims=True) + C), sp], -1)


def rope(u, cos, sin):
    u1, u2 = u[..., 0::2], u[..., 1::2]
    cos, sin = cos[None, :, None, :], sin[None, :, None, :]
    return np.stack([u1 * cos - u2 * sin, u1 * sin + u2 * cos], -1).reshape(u.shape)


def setup_inputs():
    s = mx_kscale(DIM)
    inv = 1.0 / (10000.0 ** (np.arange(0, ROPE_SP, 2) / ROPE_SP))
    ang = np.arange(S)[:, None] * inv[None, :]
    return {"x": bf(np.random.standard_normal((B, S, DIM)) * s),
            "freqs_cos": bf(np.cos(ang)),
            "freqs_sin": bf(np.sin(ang)),
            "wkv_a_w": bf(np.random.standard_normal((KV_RANK + ROPE_SP, DIM)) * 0.25 / np.sqrt(DIM) / s[None, :]),
            "wkv_a_b": bf(np.random.standard_normal(KV_RANK + ROPE_SP) * 0.1),
            "kv_norm_w": bf(np.sqrt(8.0 / KV_RANK) * (1.0 + 0.1 * np.random.standard_normal(KV_RANK))),
            "wkv_b_w": bf(np.random.standard_normal((H * (NOPE + V_SP), KV_RANK + 1)) * 0.06),
            "wkv_b_b": bf(np.random.standard_normal(H * (NOPE + V_SP)) * 0.1)}


def reference(x, freqs_cos, freqs_sin, wkv_a_w, wkv_a_b, kv_norm_w, wkv_b_w, wkv_b_b):
    kv_full = (mxq(f64(x), 2, "e4m3") @ mxq(f64(wkv_a_w), 1, "e4m3").T) + f64(wkv_a_b)
    kv, k_pe = kv_full[..., :KV_RANK], kv_full[..., KV_RANK:]
    k_pe = rope(k_pe[:, :, None, :], f64(freqs_cos), f64(freqs_sin))
    sp = kv / np.sqrt((kv * kv).mean(-1, keepdims=True) + EPS) * f64(kv_norm_w)
    t = np.sqrt((sp * sp).sum(-1, keepdims=True) + C)
    wb = f64(wkv_b_w)
    kv2 = (mxq(sp, 2, "e4m3") @ mxq(wb[:, 1:], 1, "e4m3").T) + t * wb[:, 0] + f64(wkv_b_b)
    kv2 = kv2.reshape(B, S, H, NOPE + V_SP)
    k = np.concatenate([kv2[..., :NOPE], np.broadcast_to(k_pe, (B, S, H, ROPE_SP))], -1)
    return lift(k), lift(kv2[..., NOPE:])

@@ -1,0 +1,354 @@
+from contextlib import ExitStack
+
+import concourse.mybir as mybir
+from concourse.masks import make_identity
+
+F32 = mybir.dt.float32
+BF16 = mybir.dt.bfloat16
+U32 = mybir.dt.uint32
+U8 = mybir.dt.uint8
+FP8X4 = mybir.dt.float8_e4m3fn_x4
+ALU = mybir.AluOpType
+ACT = mybir.ActivationFunctionType
+
+P = 128
+K_PASS = 512
+WORDS = K_PASS // 2
+
+TOKENS = 512
+TOKEN_TILES = TOKENS // P
+DIM = 2048
+PASSES_A = DIM // K_PASS
+KV_RANK = 512
+ROPE = 128
+A_OUT = KV_RANK + ROPE
+A_TILES = A_OUT // P
+HEADS = 16
+NOPE = 64
+V_DIM = 128
+HEAD_ROWS = NOPE + V_DIM
+B_OUT = HEADS * HEAD_ROWS
+K_COLS = HEADS * NOPE
+BANK = 512
+B_CHUNKS = B_OUT // BANK
+K_CHUNKS = K_COLS // BANK
+ROW_SLOT = 528
+EPS = 1e-6
+
+FLOPS = 2 * TOKENS * DIM * A_OUT + 2 * TOKENS * KV_RANK * B_OUT
+
+
+def tile_lorentzmla_pa_kernel(
+    tc, x, freqs_cos, freqs_sin, wkv_a_w, wkv_a_b, kv_norm_w, wkv_b_w, wkv_b_b, out_0, out_1
+):
+    nc = tc.nc
+    with ExitStack() as ctx:
+        const = ctx.enter_context(tc.tile_pool(name="const", bufs=1))
+        rows_pool = ctx.enter_context(tc.tile_pool(name="rows", bufs=5))
+        chunk_pool = ctx.enter_context(tc.tile_pool(name="chunk", bufs=3))
+        stage = ctx.enter_context(tc.tile_pool(name="stage", bufs=3))
+        work = ctx.enter_context(tc.tile_pool(name="work", bufs=2))
+        small = ctx.enter_context(tc.tile_pool(name="small", bufs=TOKEN_TILES))
+        outs = ctx.enter_context(tc.tile_pool(name="outs", bufs=TOKEN_TILES))
+        turn_psum = ctx.enter_context(tc.psum_pool(name="turn_psum", bufs=3))
+        acc_psum = ctx.enter_context(tc.psum_pool(name="acc_psum", bufs=3))
+        pe_psum = ctx.enter_context(tc.psum_pool(name="pe_psum", bufs=1))
+        misc_psum = ctx.enter_context(tc.psum_pool(name="misc_psum", bufs=1))
+
+        ident_f32 = const.tile([P, P], F32)
+        make_identity(nc, ident_f32[:])
+        ident_bf = const.tile([P, P], BF16)
+        make_identity(nc, ident_bf[:])
+        one_col = const.tile([P, 1], F32)
+        nc.vector.memset(one_col[:], 1.0)
+        eps_col = const.tile([P, 1], F32)
+        nc.vector.memset(eps_col[:], EPS)
+        warm = const.tile([P, 1], F32)
+        nc.scalar.activation(out=warm[:], in_=one_col[:], func=ACT.Sqrt)
+
+        B_ROW0, A_ROW0, G_ROW0 = 0, 32, 64
+        vec_rows = const.tile([P, P], BF16)
+        nc.vector.memset(vec_rows[:], 0.0)
+        nc.sync.dma_start(
+            out=vec_rows[A_ROW0 : A_ROW0 + A_OUT // P, :], in_=wkv_a_b.rearrange("(r c) -> r c", c=P)
+        )
+        nc.sync.dma_start(
+            out=vec_rows[G_ROW0 : G_ROW0 + KV_RANK // P, :], in_=kv_norm_w.rearrange("(r c) -> r c", c=P)
+        )
+        nc.sync.dma_start(
+            out=vec_rows[B_ROW0 : B_ROW0 + B_OUT // P, :], in_=wkv_b_b.rearrange("(r c) -> r c", c=P)
+        )
+        cos_sb = const.tile([P, 2, ROPE // 2], BF16)
+        nc.sync.dma_start(out=cos_sb[:], in_=freqs_cos.rearrange("(h p) j -> p h j", p=P))
+        sin_sb = const.tile([P, 2, ROPE // 2], BF16)
+        nc.sync.dma_start(out=sin_sb[:], in_=freqs_sin.rearrange("(h p) j -> p h j", p=P))
+
+        def spread_rows(first_row, n_rows):
+            spread = misc_psum.tile([P, 2 * BANK], BF16, tag="misc")
+            for r in range(n_rows):
+                nc.tensor.matmul(
+                    out=spread[:, P * r : P * r + P],
+                    lhsT=ident_bf[:, first_row + r : first_row + r + 1].to_broadcast([P, P]),
+                    rhs=vec_rows[:],
+                    start=True,
+                    stop=True,
+                )
+            return spread
+
+        bias_a = const.tile([P, A_OUT], BF16)
+        spread_a = spread_rows(A_ROW0, A_OUT // P)
+        nc.vector.tensor_copy(
+            out=bias_a[:, 0:KV_RANK].rearrange("p (u e q) -> p u e q", u=2, e=2),
+            in_=spread_a[:, 0:KV_RANK].rearrange("p (u q e) -> p u e q", u=2, e=2),
+        )
+        nc.vector.tensor_copy(out=bias_a[:, KV_RANK:A_OUT], in_=spread_a[:, KV_RANK:A_OUT])
+        gain = const.tile([P, KV_RANK], BF16)
+        spread_g = spread_rows(G_ROW0, KV_RANK // P)
+        nc.vector.tensor_copy(
+            out=gain[:].rearrange("p (u e q) -> p u e q", u=2, e=2),
+            in_=spread_g[:, 0:KV_RANK].rearrange("p (u q e) -> p u e q", u=2, e=2),
+        )
+        bias_b = const.tile([P, HEADS, HEAD_ROWS], BF16)
+        bias_b_flat = bias_b[:].rearrange("p h f -> p (h f)")
+        ROWS_PER_SPREAD = 2 * BANK // P
+        for s in range(B_OUT // (2 * BANK)):
+            spread_b = spread_rows(B_ROW0 + ROWS_PER_SPREAD * s, ROWS_PER_SPREAD)
+            nc.vector.tensor_copy(out=bias_b_flat[:, 2 * BANK * s : 2 * BANK * (s + 1)], in_=spread_b[:])
+
+        def regroup(sources):
+            grouped = stage.tile([P, 4, P, 2], F32, align_bytes=64)
+            for half in range(2):
+                turned = turn_psum.tile([P, 2, 2, P], F32)
+                for s in range(2):
+                    for u in range(2):
+                        nc.tensor.transpose(
+                            turned[:, s, u, :], sources[2 * half + s][:, P * u : P * u + P], ident_f32[:]
+                        )
+                nc.scalar.copy(
+                    out=grouped[:, 2 * half : 2 * half + 2], in_=turned[:].rearrange("p s u r -> p s r u")
+                )
+            return grouped
+
+        def load_rows(dram_rows):
+            rows = rows_pool.tile([P, DIM], BF16)
+            nc.sync.dma_start(out=rows[:], in_=dram_rows)
+            words = rows[:].bitcast(F32)
+            return [words[:, WORDS * g : WORDS * (g + 1)] for g in range(PASSES_A)]
+
+        wa_codes = const.tile([P, PASSES_A, A_OUT], U32, align_bytes=64)
+        wa_scales = const.tile([P, PASSES_A, A_OUT], U8, align_bytes=64)
+        kv_rows = wkv_a_w[0:KV_RANK, :].rearrange("(u q e) k -> u e q k", u=2, e=2)
+        for j in range(A_TILES):
+            if j < KV_RANK // P:
+                dram_rows = kv_rows[j // 2, j % 2]
+            else:
+                dram_rows = wkv_a_w[KV_RANK:A_OUT, :]
+            grouped = regroup(load_rows(dram_rows))
+            for g in range(PASSES_A):
+                nc.vector.quantize_mx(
+                    out=wa_codes[:, g, P * j : P * j + P].bitcast(FP8X4),
+                    scales=wa_scales[:, g, P * j : P * j + P],
+                    in_=grouped[:, g].rearrange("p r u -> p (r u)").bitcast(BF16),
+                )
+
+        x_codes = const.tile([P, TOKEN_TILES, PASSES_A * P], U32, align_bytes=64)
+        x_scales = const.tile([P, TOKEN_TILES, PASSES_A * P], U8, align_bytes=64)
+        sp_codes = const.tile([P, TOKEN_TILES, P], U32, align_bytes=64)
+        sp_scales = const.tile([P, TOKEN_TILES, P], U8, align_bytes=64)
+        x_rows = x.rearrange("b s k -> (b s) k")
+        time_t = []
+        k_outs = []
+        pe_norms = []
+        for i in range(TOKEN_TILES):
+            grouped = regroup(load_rows(x_rows[P * i : P * i + P, :]))
+            nc.vector.quantize_mx(
+                out=x_codes[:, i, :].bitcast(FP8X4),
+                scales=x_scales[:, i, :],
+                in_=grouped[:].rearrange("p g r u -> p (g r u)").bitcast(BF16),
+            )
+
+            kv_ps = acc_psum.tile([P, BANK], F32, tag="acc")
+            pe_ps = pe_psum.tile([P, ROPE], F32)
+            for out_ps, cols in ((kv_ps, slice(0, KV_RANK)), (pe_ps, slice(KV_RANK, A_OUT))):
+                for g in range(PASSES_A):
+                    nc.tensor.matmul_mx(
+                        out=out_ps[:],
+                        lhsT=x_codes[:, i, P * g : P * g + P].bitcast(FP8X4),
+                        lhsT_scale=x_scales[:, i, P * g : P * g + P],
+                        rhs=wa_codes[:, g, cols].bitcast(FP8X4),
+                        rhs_scale=wa_scales[:, g, cols],
+                        start=(g == 0),
+                        stop=(g == PASSES_A - 1),
+                    )
+            a_sb = work.tile([P, A_OUT], F32)
+            nc.vector.tensor_tensor(out=a_sb[:, 0:KV_RANK], in0=kv_ps[:], in1=bias_a[:, 0:KV_RANK], op=ALU.add)
+            nc.vector.tensor_tensor(
+                out=a_sb[:, KV_RANK:A_OUT], in0=pe_ps[:], in1=bias_a[:, KV_RANK:A_OUT], op=ALU.add
+            )
+
+            squares = work.tile([P, 2 * KV_RANK + ROPE], F32)
+            sum_kv2 = small.tile([P, 1], F32)
+            nc.scalar.activation(
+                out=squares[:, 0:KV_RANK], in_=a_sb[:, 0:KV_RANK], func=ACT.Square, accum_out=sum_kv2[:]
+            )
+            gained = work.tile([P, KV_RANK], F32)
+            nc.vector.tensor_tensor(out=gained[:], in0=a_sb[:, 0:KV_RANK], in1=gain[:], op=ALU.mult)
+            sum_gained2 = small.tile([P, 1], F32)
+            nc.scalar.activation(
+                out=squares[:, KV_RANK : 2 * KV_RANK], in_=gained[:], func=ACT.Square, accum_out=sum_gained2[:]
+            )
+            rms = small.tile([P, 1], F32)
+            nc.scalar.activation(out=rms[:], in_=sum_kv2[:], func=ACT.Sqrt, bias=eps_col[:], scale=1.0 / KV_RANK)
+            inv_rms = small.tile([P, 1], F32)
+            nc.vector.reciprocal(out=inv_rms[:], in_=rms[:])
+            sum_sp2 = small.tile([P, 1], F32)
+            nc.vector.tensor_scalar(
+                out=sum_sp2[:], in0=sum_gained2[:], scalar1=inv_rms[:], scalar2=inv_rms[:], op0=ALU.mult, op1=ALU.mult
+            )
+            t_col = small.tile([P, 1], F32)
+            nc.scalar.activation(out=t_col[:], in_=sum_sp2[:], func=ACT.Sqrt, bias=one_col[:], scale=1.0)
+            time_t.append(t_col)
+            sp_bf = work.tile([P, KV_RANK], BF16)
+            nc.scalar.activation(out=sp_bf[:], in_=gained[:], func=ACT.Copy, scale=inv_rms[:])
+
+            sp_turned = misc_psum.tile([P, 4, P], BF16, tag="misc")
+            for t in range(4):
+                nc.tensor.transpose(sp_turned[:, t, :], sp_bf[:, P * t : P * t + P], ident_bf[:])
+            sp_grouped = work.tile([P, P, 4], BF16, align_bytes=64)
+            nc.vector.tensor_copy(out=sp_grouped[:], in_=sp_turned[:].rearrange("p t r -> p r t"))
+            nc.vector.quantize_mx(
+                out=sp_codes[:, i, :].bitcast(FP8X4),
+                scales=sp_scales[:, i, :],
+                in_=sp_grouped[:].rearrange("p r t -> p (r t)"),
+            )
+
+            pe = a_sb[:, KV_RANK:A_OUT].rearrange("p (j two) -> p j two", two=2)
+            cos = cos_sb[:, i % 2, :]
+            sin = sin_sb[:, i % 2, :]
+            even_cos = work.tile([P, ROPE // 2], F32)
+            nc.gpsimd.tensor_tensor(out=even_cos[:], in0=pe[:, :, 0], in1=cos, op=ALU.mult)
+            odd_sin = work.tile([P, ROPE // 2], F32)
+            nc.gpsimd.tensor_tensor(out=odd_sin[:], in0=pe[:, :, 1], in1=sin, op=ALU.mult)
+            even_sin = work.tile([P, ROPE // 2], F32)
+            nc.gpsimd.tensor_tensor(out=even_sin[:], in0=pe[:, :, 0], in1=sin, op=ALU.mult)
+            odd_cos = work.tile([P, ROPE // 2], F32)
+            nc.gpsimd.tensor_tensor(out=odd_cos[:], in0=pe[:, :, 1], in1=cos, op=ALU.mult)
+            k_pe = work.tile([P, ROPE // 2, 2], F32)
+            nc.gpsimd.tensor_tensor(out=k_pe[:, :, 0], in0=even_cos[:], in1=odd_sin[:], op=ALU.subtract)
+            nc.gpsimd.tensor_tensor(out=k_pe[:, :, 1], in0=even_sin[:], in1=odd_cos[:], op=ALU.add)
+            k_out = outs.tile([P, HEADS, 1 + NOPE + ROPE], F32)
+            k_outs.append(k_out)
+            nc.gpsimd.tensor_scalar(
+                out=k_out[:, :, 1 + NOPE :],
+                in0=k_pe[:].rearrange("p j two -> p (j two)").unsqueeze(1).to_broadcast([P, HEADS, ROPE]),
+                scalar1=1.0,
+                scalar2=0.0,
+                op0=ALU.mult,
+                op1=ALU.add,
+            )
+            sum_pe2 = small.tile([P, 1], F32)
+            nc.scalar.activation(
+                out=squares[:, 2 * KV_RANK :], in_=k_out[:, 0, 1 + NOPE :], func=ACT.Square, accum_out=sum_pe2[:]
+            )
+            pe_norm = small.tile([P, 1], F32)
+            nc.gpsimd.tensor_scalar(
+                out=pe_norm[:], in0=sum_pe2[:], scalar1=1.0, scalar2=1.0, op0=ALU.mult, op1=ALU.add
+            )
+            pe_norms.append(pe_norm)
+
+        wb_codes = const.tile([P, B_OUT], U32, align_bytes=64)
+        wb_scales = const.tile([P, B_OUT], U8, align_bytes=64)
+        w0_all = const.tile([P, B_OUT], BF16)
+        by_head = wkv_b_w.rearrange("(h f) c -> f h c", f=HEAD_ROWS)
+        for c in range(B_CHUNKS):
+            chunk = chunk_pool.tile([P, 4, ROW_SLOT], BF16)
+            if c < K_CHUNKS:
+                for two in range(2):
+                    nc.sync.dma_start(
+                        out=chunk[NOPE * two : NOPE * (two + 1), :, 1 : 1 + KV_RANK + 1],
+                        in_=by_head[0:NOPE, 8 * c + two : 8 * (c + 1) : 2, :],
+                    )
+            else:
+                h0 = 4 * (c - K_CHUNKS)
+                nc.sync.dma_start(out=chunk[:, :, 1 : 1 + KV_RANK + 1], in_=by_head[NOPE:HEAD_ROWS, h0 : h0 + 4, :])
+            words = chunk[:].bitcast(F32)
+            grouped = regroup([words[:, m, 1 : 1 + WORDS] for m in range(4)])
+            cols = slice(BANK * c, BANK * (c + 1))
+            nc.vector.quantize_mx(
+                out=wb_codes[:, cols].bitcast(FP8X4),
+                scales=wb_scales[:, cols],
+                in_=grouped[:].rearrange("p m r u -> p (m r u)").bitcast(BF16),
+            )
+            w0_ps = misc_psum.tile([P, BANK], BF16, tag="misc")
+            for m in range(4):
+                nc.tensor.matmul(
+                    out=w0_ps[:, P * m : P * m + P],
+                    lhsT=chunk[:, m, 1:2].to_broadcast([P, P]),
+                    rhs=ident_bf[:],
+                    start=True,
+                    stop=True,
+                )
+            nc.vector.tensor_copy(out=w0_all[:, cols], in_=w0_ps[:])
+
+        k_rows = out_0.rearrange("b s h c -> (b s) (h c)")
+        v_rows = out_1.rearrange("b s h c -> (b s) (h c)")
+        for i in range(TOKEN_TILES):
+            k_out = k_outs[i]
+            v_out = outs.tile([P, HEADS, 1 + V_DIM], F32)
+            k_part = work.tile([P, HEADS, NOPE], F32)
+            for c in range(B_CHUNKS):
+                cols = slice(BANK * c, BANK * (c + 1))
+                y_ps = acc_psum.tile([P, BANK], F32, tag="acc")
+                nc.tensor.matmul_mx(
+                    out=y_ps[:],
+                    lhsT=sp_codes[:, i, :].bitcast(FP8X4),
+                    lhsT_scale=sp_scales[:, i, :],
+                    rhs=wb_codes[:, cols].bitcast(FP8X4),
+                    rhs_scale=wb_scales[:, cols],
+                    start=True,
+                    stop=True,
+                )
+                if c < K_CHUNKS:
+                    dest = k_part[:, 8 * c : 8 * (c + 1), :]
+                    width = NOPE
+                else:
+                    h0 = 4 * (c - K_CHUNKS)
+                    dest = v_out[:, h0 : h0 + 4, 1:]
+                    width = V_DIM
+                nc.vector.scalar_tensor_tensor(
+                    out=dest,
+                    in0=w0_all[:, cols].rearrange("p (h f) -> p h f", f=width),
+                    scalar=time_t[i][:],
+                    in1=y_ps[:].rearrange("p (h f) -> p h f", f=width),
+                    op0=ALU.mult,
+                    op1=ALU.add,
+                )
+            nc.gpsimd.tensor_tensor(out=k_out[:, :, 1 : 1 + NOPE], in0=k_part[:], in1=bias_b[:, :, 0:NOPE], op=ALU.add)
+            for h0 in range(0, HEADS, 4):
+                nc.vector.tensor_tensor(
+                    out=v_out[:, h0 : h0 + 4, 1:],
+                    in0=v_out[:, h0 : h0 + 4, 1:],
+                    in1=bias_b[:, h0 : h0 + 4, NOPE:],
+                    op=ALU.add,
+                )
+            head_squares = work.tile([P, B_OUT], F32, bufs=1)
+            sum_k2 = small.tile([P, HEADS], F32)
+            sum_v2 = small.tile([P, HEADS], F32)
+            for h in range(HEADS):
+                nc.scalar.activation(
+                    out=head_squares[:, K_COLS + V_DIM * h : K_COLS + V_DIM * (h + 1)],
+                    in_=v_out[:, h, 1:],
+                    func=ACT.Square,
+                    accum_out=sum_v2[:, h : h + 1],
+                )
+            nc.scalar.activation(out=v_out[:, :, 0], in_=sum_v2[:], func=ACT.Sqrt, bias=one_col[:], scale=1.0)
+            nc.sync.dma_start(out=v_rows[P * i : P * i + P, :], in_=v_out[:].rearrange("p h c -> p (h c)"))
+            for h in range(HEADS):
+                nc.scalar.activation(
+                    out=head_squares[:, NOPE * h : NOPE * (h + 1)],
+                    in_=k_out[:, h, 1 : 1 + NOPE],
+                    func=ACT.Square,
+                    accum_out=sum_k2[:, h : h + 1],
+                )
+            nc.scalar.activation(out=k_out[:, :, 0], in_=sum_k2[:], func=ACT.Sqrt, bias=pe_norms[i][:], scale=1.0)
+            nc.sync.dma_start(out=k_rows[P * i : P * i + P, :], in_=k_out[:].rearrange("p h c -> p (h c)"))

@@ -51,9 +51,8 @@ def tile_lorentzmla_pa_kernel(
         small = ctx.enter_context(tc.tile_pool(name="small", bufs=TOKEN_TILES))
         outs = ctx.enter_context(tc.tile_pool(name="outs", bufs=TOKEN_TILES))
         turn_psum = ctx.enter_context(tc.psum_pool(name="turn_psum", bufs=3))
-        acc_psum = ctx.enter_context(tc.psum_pool(name="acc_psum", bufs=3))
+        acc_psum = ctx.enter_context(tc.psum_pool(name="acc_psum", bufs=4))
         pe_psum = ctx.enter_context(tc.psum_pool(name="pe_psum", bufs=1))
-        misc_psum = ctx.enter_context(tc.psum_pool(name="misc_psum", bufs=1))
 
         ident_f32 = const.tile([P, P], F32)
         make_identity(nc, ident_f32[:])
@@ -84,7 +83,7 @@ def tile_lorentzmla_pa_kernel(
         nc.sync.dma_start(out=sin_sb[:], in_=freqs_sin.rearrange("(h p) j -> p h j", p=P))
 
         def spread_rows(first_row, n_rows):
-            spread = misc_psum.tile([P, 2 * BANK], BF16, tag="misc")
+            spread = turn_psum.tile([P, 2 * BANK], BF16, tag="turned")
             for r in range(n_rows):
                 nc.tensor.matmul(
                     out=spread[:, P * r : P * r + P],
@@ -118,7 +117,7 @@ def tile_lorentzmla_pa_kernel(
         def regroup(sources):
             grouped = stage.tile([P, 4, P, 2], F32, align_bytes=64)
             for half in range(2):
-                turned = turn_psum.tile([P, 2, 2, P], F32)
+                turned = turn_psum.tile([P, 2, 2, P], F32, tag="turned")
                 for s in range(2):
                     for u in range(2):
                         nc.tensor.transpose(
@@ -156,9 +155,6 @@ def tile_lorentzmla_pa_kernel(
         sp_codes = const.tile([P, TOKEN_TILES, P], U32, align_bytes=64)
         sp_scales = const.tile([P, TOKEN_TILES, P], U8, align_bytes=64)
         x_rows = x.rearrange("b s k -> (b s) k")
-        time_t = []
-        k_outs = []
-        pe_norms = []
         for i in range(TOKEN_TILES):
             grouped = regroup(load_rows(x_rows[P * i : P * i + P, :]))
             nc.vector.quantize_mx(
@@ -167,12 +163,20 @@ def tile_lorentzmla_pa_kernel(
                 in_=grouped[:].rearrange("p g r u -> p (g r u)").bitcast(BF16),
             )
 
+        kv_all = const.tile([P, TOKEN_TILES, KV_RANK], F32)
+        pe_all = const.tile([P, TOKEN_TILES, ROPE], F32)
+        gained = const.tile([P, TOKEN_TILES, KV_RANK], F32)
+        junk_kv = const.tile([P, 2, KV_RANK], BF16)
+        junk_gained = const.tile([P, 2, KV_RANK], BF16)
+        sum_kv2 = const.tile([P, TOKEN_TILES], F32)
+        sum_gained2 = const.tile([P, TOKEN_TILES], F32)
+        pe_ps = pe_psum.tile([P, TOKEN_TILES, ROPE], F32)
+        for i in range(TOKEN_TILES):
             kv_ps = acc_psum.tile([P, BANK], F32, tag="acc")
-            pe_ps = pe_psum.tile([P, ROPE], F32)
-            for out_ps, cols in ((kv_ps, slice(0, KV_RANK)), (pe_ps, slice(KV_RANK, A_OUT))):
+            for out_ps, cols in ((kv_ps[:], slice(0, KV_RANK)), (pe_ps[:, i, :], slice(KV_RANK, A_OUT))):
                 for g in range(PASSES_A):
                     nc.tensor.matmul_mx(
-                        out=out_ps[:],
+                        out=out_ps,
                         lhsT=x_codes[:, i, P * g : P * g + P].bitcast(FP8X4),
                         lhsT_scale=x_scales[:, i, P * g : P * g + P],
                         rhs=wa_codes[:, g, cols].bitcast(FP8X4),
@@ -180,81 +184,106 @@ def tile_lorentzmla_pa_kernel(
                         start=(g == 0),
                         stop=(g == PASSES_A - 1),
                     )
-            a_sb = work.tile([P, A_OUT], F32)
-            nc.vector.tensor_tensor(out=a_sb[:, 0:KV_RANK], in0=kv_ps[:], in1=bias_a[:, 0:KV_RANK], op=ALU.add)
-            nc.vector.tensor_tensor(
-                out=a_sb[:, KV_RANK:A_OUT], in0=pe_ps[:], in1=bias_a[:, KV_RANK:A_OUT], op=ALU.add
+            nc.vector.tensor_tensor(out=kv_all[:, i, :], in0=kv_ps[:], in1=bias_a[:, 0:KV_RANK], op=ALU.add)
+            nc.scalar.activation(
+                out=junk_kv[:, i % 2, :], in_=kv_all[:, i, :], func=ACT.Square, accum_out=sum_kv2[:, i : i + 1]
             )
+            nc.vector.tensor_tensor(out=gained[:, i, :], in0=kv_all[:, i, :], in1=gain[:], op=ALU.mult)
+            nc.scalar.activation(
+                out=junk_gained[:, i % 2, :],
+                in_=gained[:, i, :],
+                func=ACT.Square,
+                accum_out=sum_gained2[:, i : i + 1],
+            )
+        nc.vector.tensor_tensor(
+            out=pe_all[:],
+            in0=pe_ps[:],
+            in1=bias_a[:, KV_RANK:A_OUT].unsqueeze(1).to_broadcast([P, TOKEN_TILES, ROPE]),
+            op=ALU.add,
+        )
 
-            squares = work.tile([P, 2 * KV_RANK + ROPE], F32)
-            sum_kv2 = small.tile([P, 1], F32)
-            nc.scalar.activation(
-                out=squares[:, 0:KV_RANK], in_=a_sb[:, 0:KV_RANK], func=ACT.Square, accum_out=sum_kv2[:]
-            )
-            gained = work.tile([P, KV_RANK], F32)
-            nc.vector.tensor_tensor(out=gained[:], in0=a_sb[:, 0:KV_RANK], in1=gain[:], op=ALU.mult)
-            sum_gained2 = small.tile([P, 1], F32)
-            nc.scalar.activation(
-                out=squares[:, KV_RANK : 2 * KV_RANK], in_=gained[:], func=ACT.Square, accum_out=sum_gained2[:]
-            )
-            rms = small.tile([P, 1], F32)
-            nc.scalar.activation(out=rms[:], in_=sum_kv2[:], func=ACT.Sqrt, bias=eps_col[:], scale=1.0 / KV_RANK)
-            inv_rms = small.tile([P, 1], F32)
-            nc.vector.reciprocal(out=inv_rms[:], in_=rms[:])
-            sum_sp2 = small.tile([P, 1], F32)
+        rms = const.tile([P, TOKEN_TILES], F32)
+        nc.scalar.activation(out=rms[:], in_=sum_kv2[:], func=ACT.Sqrt, bias=eps_col[:], scale=1.0 / KV_RANK)
+        inv_rms = const.tile([P, TOKEN_TILES], F32)
+        nc.vector.reciprocal(out=inv_rms[:], in_=rms[:])
+        sp_bf = const.tile([P, TOKEN_TILES, KV_RANK], BF16)
+        for i in range(TOKEN_TILES):
             nc.vector.tensor_scalar(
-                out=sum_sp2[:], in0=sum_gained2[:], scalar1=inv_rms[:], scalar2=inv_rms[:], op0=ALU.mult, op1=ALU.mult
+                out=sp_bf[:, i, :], in0=gained[:, i, :], scalar1=inv_rms[:, i : i + 1], scalar2=None, op0=ALU.mult
             )
-            t_col = small.tile([P, 1], F32)
-            nc.scalar.activation(out=t_col[:], in_=sum_sp2[:], func=ACT.Sqrt, bias=one_col[:], scale=1.0)
-            time_t.append(t_col)
-            sp_bf = work.tile([P, KV_RANK], BF16)
-            nc.scalar.activation(out=sp_bf[:], in_=gained[:], func=ACT.Copy, scale=inv_rms[:])
+        sum_sp2 = const.tile([P, TOKEN_TILES], F32)
+        nc.vector.tensor_tensor(out=sum_sp2[:], in0=sum_gained2[:], in1=inv_rms[:], op=ALU.mult)
+        nc.vector.tensor_tensor(out=sum_sp2[:], in0=sum_sp2[:], in1=inv_rms[:], op=ALU.mult)
+        time_t = const.tile([P, TOKEN_TILES], F32)
+        nc.scalar.activation(out=time_t[:], in_=sum_sp2[:], func=ACT.Sqrt, bias=one_col[:], scale=1.0)
 
-            sp_turned = misc_psum.tile([P, 4, P], BF16, tag="misc")
-            for t in range(4):
-                nc.tensor.transpose(sp_turned[:, t, :], sp_bf[:, P * t : P * t + P], ident_bf[:])
-            sp_grouped = work.tile([P, P, 4], BF16, align_bytes=64)
-            nc.vector.tensor_copy(out=sp_grouped[:], in_=sp_turned[:].rearrange("p t r -> p r t"))
-            nc.vector.quantize_mx(
-                out=sp_codes[:, i, :].bitcast(FP8X4),
-                scales=sp_scales[:, i, :],
-                in_=sp_grouped[:].rearrange("p r t -> p (r t)"),
+        sp_grouped = const.tile([P, TOKEN_TILES, P, 4], BF16, align_bytes=64)
+        for pair in range(TOKEN_TILES // 2):
+            sp_turned = turn_psum.tile([P, 2, 4, P], BF16, tag="turned")
+            for i2 in range(2):
+                for t in range(4):
+                    nc.tensor.transpose(
+                        sp_turned[:, i2, t, :], sp_bf[:, 2 * pair + i2, P * t : P * t + P], ident_bf[:]
+                    )
+            nc.vector.tensor_copy(
+                out=sp_grouped[:, 2 * pair : 2 * pair + 2], in_=sp_turned[:].rearrange("p i t r -> p i r t")
             )
+        nc.vector.quantize_mx(
+            out=sp_codes[:].rearrange("p i r -> p (i r)").bitcast(FP8X4),
+            scales=sp_scales[:].rearrange("p i r -> p (i r)"),
+            in_=sp_grouped[:].rearrange("p i r t -> p (i r t)"),
+        )
 
-            pe = a_sb[:, KV_RANK:A_OUT].rearrange("p (j two) -> p j two", two=2)
-            cos = cos_sb[:, i % 2, :]
-            sin = sin_sb[:, i % 2, :]
-            even_cos = work.tile([P, ROPE // 2], F32)
-            nc.gpsimd.tensor_tensor(out=even_cos[:], in0=pe[:, :, 0], in1=cos, op=ALU.mult)
-            odd_sin = work.tile([P, ROPE // 2], F32)
-            nc.gpsimd.tensor_tensor(out=odd_sin[:], in0=pe[:, :, 1], in1=sin, op=ALU.mult)
-            even_sin = work.tile([P, ROPE // 2], F32)
-            nc.gpsimd.tensor_tensor(out=even_sin[:], in0=pe[:, :, 0], in1=sin, op=ALU.mult)
-            odd_cos = work.tile([P, ROPE // 2], F32)
-            nc.gpsimd.tensor_tensor(out=odd_cos[:], in0=pe[:, :, 1], in1=cos, op=ALU.mult)
-            k_pe = work.tile([P, ROPE // 2, 2], F32)
-            nc.gpsimd.tensor_tensor(out=k_pe[:, :, 0], in0=even_cos[:], in1=odd_sin[:], op=ALU.subtract)
-            nc.gpsimd.tensor_tensor(out=k_pe[:, :, 1], in0=even_sin[:], in1=odd_cos[:], op=ALU.add)
+        HALF = ROPE // 2
+        pe_pairs = pe_all[:].rearrange("p i (j two) -> p (i j) two", two=2)
+        even = pe_pairs[:, :, 0].rearrange("p (b hj) -> p b hj", b=2)
+        odd = pe_pairs[:, :, 1].rearrange("p (b hj) -> p b hj", b=2)
+        cos = cos_sb[:].rearrange("p h j -> p (h j)").unsqueeze(1).to_broadcast([P, 2, 2 * HALF])
+        sin = sin_sb[:].rearrange("p h j -> p (h j)").unsqueeze(1).to_broadcast([P, 2, 2 * HALF])
+        even_cos = const.tile([P, 2, 2 * HALF], F32)
+        nc.gpsimd.tensor_tensor(out=even_cos[:], in0=even, in1=cos, op=ALU.mult)
+        odd_sin = const.tile([P, 2, 2 * HALF], F32)
+        nc.gpsimd.tensor_tensor(out=odd_sin[:], in0=odd, in1=sin, op=ALU.mult)
+        even_sin = const.tile([P, 2, 2 * HALF], F32)
+        nc.gpsimd.tensor_tensor(out=even_sin[:], in0=even, in1=sin, op=ALU.mult)
+        odd_cos = const.tile([P, 2, 2 * HALF], F32)
+        nc.gpsimd.tensor_tensor(out=odd_cos[:], in0=odd, in1=cos, op=ALU.mult)
+        k_pe = const.tile([P, TOKEN_TILES, ROPE], F32)
+        k_pe_pairs = k_pe[:].rearrange("p i (j two) -> p (i j) two", two=2)
+        nc.gpsimd.tensor_tensor(
+            out=k_pe_pairs[:, :, 0],
+            in0=even_cos[:].rearrange("p b hj -> p (b hj)"),
+            in1=odd_sin[:].rearrange("p b hj -> p (b hj)"),
+            op=ALU.subtract,
+        )
+        nc.gpsimd.tensor_tensor(
+            out=k_pe_pairs[:, :, 1],
+            in0=even_sin[:].rearrange("p b hj -> p (b hj)"),
+            in1=odd_cos[:].rearrange("p b hj -> p (b hj)"),
+            op=ALU.add,
+        )
+        k_outs = []
+        junk_pe = const.tile([P, 2, ROPE], BF16)
+        sum_pe2 = const.tile([P, TOKEN_TILES], F32)
+        for i in range(TOKEN_TILES):
             k_out = outs.tile([P, HEADS, 1 + NOPE + ROPE], F32)
             k_outs.append(k_out)
             nc.gpsimd.tensor_scalar(
                 out=k_out[:, :, 1 + NOPE :],
-                in0=k_pe[:].rearrange("p j two -> p (j two)").unsqueeze(1).to_broadcast([P, HEADS, ROPE]),
+                in0=k_pe[:, i, :].unsqueeze(1).to_broadcast([P, HEADS, ROPE]),
                 scalar1=1.0,
                 scalar2=0.0,
                 op0=ALU.mult,
                 op1=ALU.add,
             )
-            sum_pe2 = small.tile([P, 1], F32)
             nc.scalar.activation(
-                out=squares[:, 2 * KV_RANK :], in_=k_out[:, 0, 1 + NOPE :], func=ACT.Square, accum_out=sum_pe2[:]
+                out=junk_pe[:, i % 2, :],
+                in_=k_out[:, 0, 1 + NOPE :],
+                func=ACT.Square,
+                accum_out=sum_pe2[:, i : i + 1],
             )
-            pe_norm = small.tile([P, 1], F32)
-            nc.gpsimd.tensor_scalar(
-                out=pe_norm[:], in0=sum_pe2[:], scalar1=1.0, scalar2=1.0, op0=ALU.mult, op1=ALU.add
-            )
-            pe_norms.append(pe_norm)
+        pe_norm = const.tile([P, TOKEN_TILES], F32)
+        nc.gpsimd.tensor_scalar(out=pe_norm[:], in0=sum_pe2[:], scalar1=1.0, scalar2=1.0, op0=ALU.mult, op1=ALU.add)
 
         wb_codes = const.tile([P, B_OUT], U32, align_bytes=64)
         wb_scales = const.tile([P, B_OUT], U8, align_bytes=64)
@@ -279,7 +308,7 @@ def tile_lorentzmla_pa_kernel(
                 scales=wb_scales[:, cols],
                 in_=grouped[:].rearrange("p m r u -> p (m r u)").bitcast(BF16),
             )
-            w0_ps = misc_psum.tile([P, BANK], BF16, tag="misc")
+            w0_ps = turn_psum.tile([P, BANK], BF16, tag="turned")
             for m in range(4):
                 nc.tensor.matmul(
                     out=w0_ps[:, P * m : P * m + P],
@@ -292,6 +321,7 @@ def tile_lorentzmla_pa_kernel(
 
         k_rows = out_0.rearrange("b s h c -> (b s) (h c)")
         v_rows = out_1.rearrange("b s h c -> (b s) (h c)")
+        junk_head = const.tile([P, 4, V_DIM], BF16)
         for i in range(TOKEN_TILES):
             k_out = k_outs[i]
             v_out = outs.tile([P, HEADS, 1 + V_DIM], F32)
@@ -318,7 +348,7 @@ def tile_lorentzmla_pa_kernel(
                 nc.vector.scalar_tensor_tensor(
                     out=dest,
                     in0=w0_all[:, cols].rearrange("p (h f) -> p h f", f=width),
-                    scalar=time_t[i][:],
+                    scalar=time_t[:, i : i + 1],
                     in1=y_ps[:].rearrange("p (h f) -> p h f", f=width),
                     op0=ALU.mult,
                     op1=ALU.add,
@@ -331,12 +361,11 @@ def tile_lorentzmla_pa_kernel(
                     in1=bias_b[:, h0 : h0 + 4, NOPE:],
                     op=ALU.add,
                 )
-            head_squares = work.tile([P, B_OUT], F32, bufs=1)
             sum_k2 = small.tile([P, HEADS], F32)
             sum_v2 = small.tile([P, HEADS], F32)
             for h in range(HEADS):
                 nc.scalar.activation(
-                    out=head_squares[:, K_COLS + V_DIM * h : K_COLS + V_DIM * (h + 1)],
+                    out=junk_head[:, h % 4, :],
                     in_=v_out[:, h, 1:],
                     func=ACT.Square,
                     accum_out=sum_v2[:, h : h + 1],
@@ -345,10 +374,10 @@ def tile_lorentzmla_pa_kernel(
             nc.sync.dma_start(out=v_rows[P * i : P * i + P, :], in_=v_out[:].rearrange("p h c -> p (h c)"))
             for h in range(HEADS):
                 nc.scalar.activation(
-                    out=head_squares[:, NOPE * h : NOPE * (h + 1)],
+                    out=junk_head[:, h % 4, 0:NOPE],
                     in_=k_out[:, h, 1 : 1 + NOPE],
                     func=ACT.Square,
                     accum_out=sum_k2[:, h : h + 1],
                 )
-            nc.scalar.activation(out=k_out[:, :, 0], in_=sum_k2[:], func=ACT.Sqrt, bias=pe_norms[i][:], scale=1.0)
+            nc.scalar.activation(out=k_out[:, :, 0], in_=sum_k2[:], func=ACT.Sqrt, bias=pe_norm[:, i : i + 1], scale=1.0)
             nc.sync.dma_start(out=k_rows[P * i : P * i + P, :], in_=k_out[:].rearrange("p h c -> p (h c)"))

@@ -241,22 +241,22 @@ def tile_lorentzmla_pa_kernel(
         cos = cos_sb[:].rearrange("p h j -> p (h j)").unsqueeze(1).to_broadcast([P, 2, 2 * HALF])
         sin = sin_sb[:].rearrange("p h j -> p (h j)").unsqueeze(1).to_broadcast([P, 2, 2 * HALF])
         even_cos = const.tile([P, 2, 2 * HALF], F32)
-        nc.gpsimd.tensor_tensor(out=even_cos[:], in0=even, in1=cos, op=ALU.mult)
+        nc.vector.tensor_tensor(out=even_cos[:], in0=even, in1=cos, op=ALU.mult)
         odd_sin = const.tile([P, 2, 2 * HALF], F32)
-        nc.gpsimd.tensor_tensor(out=odd_sin[:], in0=odd, in1=sin, op=ALU.mult)
+        nc.vector.tensor_tensor(out=odd_sin[:], in0=odd, in1=sin, op=ALU.mult)
         even_sin = const.tile([P, 2, 2 * HALF], F32)
-        nc.gpsimd.tensor_tensor(out=even_sin[:], in0=even, in1=sin, op=ALU.mult)
+        nc.vector.tensor_tensor(out=even_sin[:], in0=even, in1=sin, op=ALU.mult)
         odd_cos = const.tile([P, 2, 2 * HALF], F32)
-        nc.gpsimd.tensor_tensor(out=odd_cos[:], in0=odd, in1=cos, op=ALU.mult)
+        nc.vector.tensor_tensor(out=odd_cos[:], in0=odd, in1=cos, op=ALU.mult)
         k_pe = const.tile([P, TOKEN_TILES, ROPE], F32)
         k_pe_pairs = k_pe[:].rearrange("p i (j two) -> p (i j) two", two=2)
-        nc.gpsimd.tensor_tensor(
+        nc.vector.tensor_tensor(
             out=k_pe_pairs[:, :, 0],
             in0=even_cos[:].rearrange("p b hj -> p (b hj)"),
             in1=odd_sin[:].rearrange("p b hj -> p (b hj)"),
             op=ALU.subtract,
         )
-        nc.gpsimd.tensor_tensor(
+        nc.vector.tensor_tensor(
             out=k_pe_pairs[:, :, 1],
             in0=even_sin[:].rearrange("p b hj -> p (b hj)"),
             in1=odd_cos[:].rearrange("p b hj -> p (b hj)"),
@@ -268,13 +268,8 @@ def tile_lorentzmla_pa_kernel(
         for i in range(TOKEN_TILES):
             k_out = outs.tile([P, HEADS, 1 + NOPE + ROPE], F32)
             k_outs.append(k_out)
-            nc.gpsimd.tensor_scalar(
-                out=k_out[:, :, 1 + NOPE :],
-                in0=k_pe[:, i, :].unsqueeze(1).to_broadcast([P, HEADS, ROPE]),
-                scalar1=1.0,
-                scalar2=0.0,
-                op0=ALU.mult,
-                op1=ALU.add,
+            nc.vector.tensor_copy(
+                out=k_out[:, :, 1 + NOPE :], in_=k_pe[:, i, :].unsqueeze(1).to_broadcast([P, HEADS, ROPE])
             )
             nc.scalar.activation(
                 out=junk_pe[:, i % 2, :],
@@ -283,7 +278,7 @@ def tile_lorentzmla_pa_kernel(
                 accum_out=sum_pe2[:, i : i + 1],
             )
         pe_norm = const.tile([P, TOKEN_TILES], F32)
-        nc.gpsimd.tensor_scalar(out=pe_norm[:], in0=sum_pe2[:], scalar1=1.0, scalar2=1.0, op0=ALU.mult, op1=ALU.add)
+        nc.vector.tensor_scalar(out=pe_norm[:], in0=sum_pe2[:], scalar1=1.0, scalar2=1.0, op0=ALU.mult, op1=ALU.add)
 
         wb_codes = const.tile([P, B_OUT], U32, align_bytes=64)
         wb_scales = const.tile([P, B_OUT], U8, align_bytes=64)
@@ -353,7 +348,7 @@ def tile_lorentzmla_pa_kernel(
                     op0=ALU.mult,
                     op1=ALU.add,
                 )
-            nc.gpsimd.tensor_tensor(out=k_out[:, :, 1 : 1 + NOPE], in0=k_part[:], in1=bias_b[:, :, 0:NOPE], op=ALU.add)
+            nc.vector.tensor_tensor(out=k_out[:, :, 1 : 1 + NOPE], in0=k_part[:], in1=bias_b[:, :, 0:NOPE], op=ALU.add)
             for h0 in range(0, HEADS, 4):
                 nc.vector.tensor_tensor(
                     out=v_out[:, h0 : h0 + 4, 1:],

@@ -241,22 +241,22 @@ def tile_lorentzmla_pa_kernel(
         cos = cos_sb[:].rearrange("p h j -> p (h j)").unsqueeze(1).to_broadcast([P, 2, 2 * HALF])
         sin = sin_sb[:].rearrange("p h j -> p (h j)").unsqueeze(1).to_broadcast([P, 2, 2 * HALF])
         even_cos = const.tile([P, 2, 2 * HALF], F32)
-        nc.vector.tensor_tensor(out=even_cos[:], in0=even, in1=cos, op=ALU.mult)
+        nc.gpsimd.tensor_tensor(out=even_cos[:], in0=even, in1=cos, op=ALU.mult)
         odd_sin = const.tile([P, 2, 2 * HALF], F32)
-        nc.vector.tensor_tensor(out=odd_sin[:], in0=odd, in1=sin, op=ALU.mult)
+        nc.gpsimd.tensor_tensor(out=odd_sin[:], in0=odd, in1=sin, op=ALU.mult)
         even_sin = const.tile([P, 2, 2 * HALF], F32)
-        nc.vector.tensor_tensor(out=even_sin[:], in0=even, in1=sin, op=ALU.mult)
+        nc.gpsimd.tensor_tensor(out=even_sin[:], in0=even, in1=sin, op=ALU.mult)
         odd_cos = const.tile([P, 2, 2 * HALF], F32)
-        nc.vector.tensor_tensor(out=odd_cos[:], in0=odd, in1=cos, op=ALU.mult)
+        nc.gpsimd.tensor_tensor(out=odd_cos[:], in0=odd, in1=cos, op=ALU.mult)
         k_pe = const.tile([P, TOKEN_TILES, ROPE], F32)
         k_pe_pairs = k_pe[:].rearrange("p i (j two) -> p (i j) two", two=2)
-        nc.vector.tensor_tensor(
+        nc.gpsimd.tensor_tensor(
             out=k_pe_pairs[:, :, 0],
             in0=even_cos[:].rearrange("p b hj -> p (b hj)"),
             in1=odd_sin[:].rearrange("p b hj -> p (b hj)"),
             op=ALU.subtract,
         )
-        nc.vector.tensor_tensor(
+        nc.gpsimd.tensor_tensor(
             out=k_pe_pairs[:, :, 1],
             in0=even_sin[:].rearrange("p b hj -> p (b hj)"),
             in1=odd_cos[:].rearrange("p b hj -> p (b hj)"),
@@ -268,8 +268,13 @@ def tile_lorentzmla_pa_kernel(
         for i in range(TOKEN_TILES):
             k_out = outs.tile([P, HEADS, 1 + NOPE + ROPE], F32)
             k_outs.append(k_out)
-            nc.vector.tensor_copy(
-                out=k_out[:, :, 1 + NOPE :], in_=k_pe[:, i, :].unsqueeze(1).to_broadcast([P, HEADS, ROPE])
+            nc.gpsimd.tensor_scalar(
+                out=k_out[:, :, 1 + NOPE :],
+                in0=k_pe[:, i, :].unsqueeze(1).to_broadcast([P, HEADS, ROPE]),
+                scalar1=1.0,
+                scalar2=0.0,
+                op0=ALU.mult,
+                op1=ALU.add,
             )
             nc.scalar.activation(
                 out=junk_pe[:, i % 2, :],
@@ -278,7 +283,7 @@ def tile_lorentzmla_pa_kernel(
                 accum_out=sum_pe2[:, i : i + 1],
             )
         pe_norm = const.tile([P, TOKEN_TILES], F32)
-        nc.vector.tensor_scalar(out=pe_norm[:], in0=sum_pe2[:], scalar1=1.0, scalar2=1.0, op0=ALU.mult, op1=ALU.add)
+        nc.gpsimd.tensor_scalar(out=pe_norm[:], in0=sum_pe2[:], scalar1=1.0, scalar2=1.0, op0=ALU.mult, op1=ALU.add)
 
         wb_codes = const.tile([P, B_OUT], U32, align_bytes=64)
         wb_scales = const.tile([P, B_OUT], U8, align_bytes=64)
@@ -316,10 +321,9 @@ def tile_lorentzmla_pa_kernel(
 
         k_rows = out_0.rearrange("b s h c -> (b s) (h c)")
         v_rows = out_1.rearrange("b s h c -> (b s) (h c)")
-        junk_head = const.tile([P, 4, V_DIM], BF16)
         for i in range(TOKEN_TILES):
             k_out = k_outs[i]
-            v_out = outs.tile([P, HEADS, 1 + V_DIM], F32)
+            v_out = outs.tile([P, HEADS, 1 + V_DIM], F32, bufs=2)
             k_part = work.tile([P, HEADS, NOPE], F32)
             for c in range(B_CHUNKS):
                 cols = slice(BANK * c, BANK * (c + 1))
@@ -348,7 +352,7 @@ def tile_lorentzmla_pa_kernel(
                     op0=ALU.mult,
                     op1=ALU.add,
                 )
-            nc.vector.tensor_tensor(out=k_out[:, :, 1 : 1 + NOPE], in0=k_part[:], in1=bias_b[:, :, 0:NOPE], op=ALU.add)
+            nc.gpsimd.tensor_tensor(out=k_out[:, :, 1 : 1 + NOPE], in0=k_part[:], in1=bias_b[:, :, 0:NOPE], op=ALU.add)
             for h0 in range(0, HEADS, 4):
                 nc.vector.tensor_tensor(
                     out=v_out[:, h0 : h0 + 4, 1:],
@@ -358,21 +362,14 @@ def tile_lorentzmla_pa_kernel(
                 )
             sum_k2 = small.tile([P, HEADS], F32)
             sum_v2 = small.tile([P, HEADS], F32)
-            for h in range(HEADS):
-                nc.scalar.activation(
-                    out=junk_head[:, h % 4, :],
-                    in_=v_out[:, h, 1:],
-                    func=ACT.Square,
-                    accum_out=sum_v2[:, h : h + 1],
-                )
+            v_squares = work.tile([P, HEADS, V_DIM], F32, bufs=1)
+            for h0 in range(0, HEADS, 4):
+                nc.scalar.activation(out=v_squares[:, h0 : h0 + 4, :], in_=v_out[:, h0 : h0 + 4, 1:], func=ACT.Square)
+            nc.vector.tensor_reduce(out=sum_v2[:], in_=v_squares[:], axis=mybir.AxisListType.X, op=ALU.add)
             nc.scalar.activation(out=v_out[:, :, 0], in_=sum_v2[:], func=ACT.Sqrt, bias=one_col[:], scale=1.0)
             nc.sync.dma_start(out=v_rows[P * i : P * i + P, :], in_=v_out[:].rearrange("p h c -> p (h c)"))
-            for h in range(HEADS):
-                nc.scalar.activation(
-                    out=junk_head[:, h % 4, 0:NOPE],
-                    in_=k_out[:, h, 1 : 1 + NOPE],
-                    func=ACT.Square,
-                    accum_out=sum_k2[:, h : h + 1],
-                )
+            k_squares = work.tile([P, HEADS, NOPE], F32, bufs=1)
+            nc.scalar.activation(out=k_squares[:], in_=k_out[:, :, 1 : 1 + NOPE], func=ACT.Square)
+            nc.vector.tensor_reduce(out=sum_k2[:], in_=k_squares[:], axis=mybir.AxisListType.X, op=ALU.add)
             nc.scalar.activation(out=k_out[:, :, 0], in_=sum_k2[:], func=ACT.Sqrt, bias=pe_norm[:, i : i + 1], scale=1.0)
             nc.sync.dma_start(out=k_rows[P * i : P * i + P, :], in_=k_out[:].rearrange("p h c -> p (h c)"))

@@ -14,6 +14,7 @@ ACT = mybir.ActivationFunctionType
 P = 128
 K_PASS = 512
 WORDS = K_PASS // 2
+BANK = 512
 
 TOKENS = 512
 TOKEN_TILES = TOKENS // P
@@ -28,10 +29,8 @@ NOPE = 64
 V_DIM = 128
 HEAD_ROWS = NOPE + V_DIM
 B_OUT = HEADS * HEAD_ROWS
-K_COLS = HEADS * NOPE
-BANK = 512
+B_TILES = B_OUT // P
 B_CHUNKS = B_OUT // BANK
-K_CHUNKS = K_COLS // BANK
 ROW_SLOT = 528
 EPS = 1e-6
 
@@ -43,76 +42,35 @@ def tile_lorentzmla_pa_kernel(
 ):
     nc = tc.nc
     with ExitStack() as ctx:
-        const = ctx.enter_context(tc.tile_pool(name="const", bufs=1))
-        rows_pool = ctx.enter_context(tc.tile_pool(name="rows", bufs=5))
-        chunk_pool = ctx.enter_context(tc.tile_pool(name="chunk", bufs=3))
+        keep = ctx.enter_context(tc.tile_pool(name="keep", bufs=1))
         stage = ctx.enter_context(tc.tile_pool(name="stage", bufs=3))
-        work = ctx.enter_context(tc.tile_pool(name="work", bufs=2))
-        small = ctx.enter_context(tc.tile_pool(name="small", bufs=TOKEN_TILES))
-        outs = ctx.enter_context(tc.tile_pool(name="outs", bufs=TOKEN_TILES))
         turn_psum = ctx.enter_context(tc.psum_pool(name="turn_psum", bufs=3))
         acc_psum = ctx.enter_context(tc.psum_pool(name="acc_psum", bufs=4))
         pe_psum = ctx.enter_context(tc.psum_pool(name="pe_psum", bufs=1))
 
-        ident_f32 = const.tile([P, P], F32)
+        wa_codes = keep.tile([P, PASSES_A, A_OUT], U32, align_bytes=64)
+        wa_scales = keep.tile([P, PASSES_A, A_OUT], U8, align_bytes=64)
+        x_codes = keep.tile([P, TOKEN_TILES, PASSES_A * P], U32, align_bytes=64)
+        x_scales = keep.tile([P, TOKEN_TILES, PASSES_A * P], U8, align_bytes=64)
+        sp_codes = keep.tile([P, TOKEN_TILES, P], U32, align_bytes=64)
+        sp_scales = keep.tile([P, TOKEN_TILES, P], U8, align_bytes=64)
+        wb_codes = keep.tile([P, B_OUT], U32, align_bytes=64)
+        wb_scales = keep.tile([P, B_OUT], U8, align_bytes=64)
+        w0_all = keep.tile([P, B_OUT], BF16)
+        bias_b = keep.tile([P, HEADS, HEAD_ROWS], BF16)
+        time_t = keep.tile([P, TOKEN_TILES], F32)
+        k_pe = keep.tile([P, TOKEN_TILES, ROPE], F32)
+
+        ident_f32 = keep.tile([P, P], F32)
         make_identity(nc, ident_f32[:])
-        ident_bf = const.tile([P, P], BF16)
+        ident_bf = keep.tile([P, P], BF16)
         make_identity(nc, ident_bf[:])
-        one_col = const.tile([P, 1], F32)
+        one_col = keep.tile([P, 1], F32)
         nc.vector.memset(one_col[:], 1.0)
-        eps_col = const.tile([P, 1], F32)
+        eps_col = keep.tile([P, 1], F32)
         nc.vector.memset(eps_col[:], EPS)
-        warm = const.tile([P, 1], F32)
+        warm = keep.tile([P, 1], F32)
         nc.scalar.activation(out=warm[:], in_=one_col[:], func=ACT.Sqrt)
-
-        B_ROW0, A_ROW0, G_ROW0 = 0, 32, 64
-        vec_rows = const.tile([P, P], BF16)
-        nc.vector.memset(vec_rows[:], 0.0)
-        nc.sync.dma_start(
-            out=vec_rows[A_ROW0 : A_ROW0 + A_OUT // P, :], in_=wkv_a_b.rearrange("(r c) -> r c", c=P)
-        )
-        nc.sync.dma_start(
-            out=vec_rows[G_ROW0 : G_ROW0 + KV_RANK // P, :], in_=kv_norm_w.rearrange("(r c) -> r c", c=P)
-        )
-        nc.sync.dma_start(
-            out=vec_rows[B_ROW0 : B_ROW0 + B_OUT // P, :], in_=wkv_b_b.rearrange("(r c) -> r c", c=P)
-        )
-        cos_sb = const.tile([P, 2, ROPE // 2], BF16)
-        nc.sync.dma_start(out=cos_sb[:], in_=freqs_cos.rearrange("(h p) j -> p h j", p=P))
-        sin_sb = const.tile([P, 2, ROPE // 2], BF16)
-        nc.sync.dma_start(out=sin_sb[:], in_=freqs_sin.rearrange("(h p) j -> p h j", p=P))
-
-        def spread_rows(first_row, n_rows):
-            spread = turn_psum.tile([P, 2 * BANK], BF16, tag="turned")
-            for r in range(n_rows):
-                nc.tensor.matmul(
-                    out=spread[:, P * r : P * r + P],
-                    lhsT=ident_bf[:, first_row + r : first_row + r + 1].to_broadcast([P, P]),
-                    rhs=vec_rows[:],
-                    start=True,
-                    stop=True,
-                )
-            return spread
-
-        bias_a = const.tile([P, A_OUT], BF16)
-        spread_a = spread_rows(A_ROW0, A_OUT // P)
-        nc.vector.tensor_copy(
-            out=bias_a[:, 0:KV_RANK].rearrange("p (u e q) -> p u e q", u=2, e=2),
-            in_=spread_a[:, 0:KV_RANK].rearrange("p (u q e) -> p u e q", u=2, e=2),
-        )
-        nc.vector.tensor_copy(out=bias_a[:, KV_RANK:A_OUT], in_=spread_a[:, KV_RANK:A_OUT])
-        gain = const.tile([P, KV_RANK], BF16)
-        spread_g = spread_rows(G_ROW0, KV_RANK // P)
-        nc.vector.tensor_copy(
-            out=gain[:].rearrange("p (u e q) -> p u e q", u=2, e=2),
-            in_=spread_g[:, 0:KV_RANK].rearrange("p (u q e) -> p u e q", u=2, e=2),
-        )
-        bias_b = const.tile([P, HEADS, HEAD_ROWS], BF16)
-        bias_b_flat = bias_b[:].rearrange("p h f -> p (h f)")
-        ROWS_PER_SPREAD = 2 * BANK // P
-        for s in range(B_OUT // (2 * BANK)):
-            spread_b = spread_rows(B_ROW0 + ROWS_PER_SPREAD * s, ROWS_PER_SPREAD)
-            nc.vector.tensor_copy(out=bias_b_flat[:, 2 * BANK * s : 2 * BANK * (s + 1)], in_=spread_b[:])
 
         def regroup(sources):
             grouped = stage.tile([P, 4, P, 2], F32, align_bytes=64)
@@ -128,248 +86,267 @@ def tile_lorentzmla_pa_kernel(
                 )
             return grouped
 
-        def load_rows(dram_rows):
-            rows = rows_pool.tile([P, DIM], BF16)
-            nc.sync.dma_start(out=rows[:], in_=dram_rows)
-            words = rows[:].bitcast(F32)
-            return [words[:, WORDS * g : WORDS * (g + 1)] for g in range(PASSES_A)]
-
-        wa_codes = const.tile([P, PASSES_A, A_OUT], U32, align_bytes=64)
-        wa_scales = const.tile([P, PASSES_A, A_OUT], U8, align_bytes=64)
-        kv_rows = wkv_a_w[0:KV_RANK, :].rearrange("(u q e) k -> u e q k", u=2, e=2)
-        for j in range(A_TILES):
-            if j < KV_RANK // P:
-                dram_rows = kv_rows[j // 2, j % 2]
-            else:
-                dram_rows = wkv_a_w[KV_RANK:A_OUT, :]
-            grouped = regroup(load_rows(dram_rows))
-            for g in range(PASSES_A):
-                nc.vector.quantize_mx(
-                    out=wa_codes[:, g, P * j : P * j + P].bitcast(FP8X4),
-                    scales=wa_scales[:, g, P * j : P * j + P],
-                    in_=grouped[:, g].rearrange("p r u -> p (r u)").bitcast(BF16),
+        with tc.tile_pool(name="front", bufs=1) as front:
+            A_ROW0, G_ROW0 = 0, 32
+            vec_rows = front.tile([P, P], BF16)
+            nc.vector.memset(vec_rows[:], 0.0)
+            nc.sync.dma_start(
+                out=vec_rows[A_ROW0 : A_ROW0 + A_TILES, :], in_=wkv_a_b.rearrange("(r c) -> r c", c=P)
+            )
+            nc.sync.dma_start(
+                out=vec_rows[G_ROW0 : G_ROW0 + KV_RANK // P, :], in_=kv_norm_w.rearrange("(r c) -> r c", c=P)
+            )
+            wa_sb = front.tile([P, A_TILES, DIM], BF16)
+            kv_rows = wkv_a_w[0:KV_RANK, :].rearrange("(u q e) k -> u e q k", u=2, e=2)
+            for j in range(KV_RANK // P):
+                nc.sync.dma_start(out=wa_sb[:, j, :], in_=kv_rows[j // 2, j % 2])
+            nc.sync.dma_start(out=wa_sb[:, KV_RANK // P, :], in_=wkv_a_w[KV_RANK:A_OUT, :])
+            x_sb = front.tile([P, TOKEN_TILES, DIM], BF16)
+            x_rows = x.rearrange("b s k -> (b s) k")
+            for i in range(TOKEN_TILES):
+                nc.sync.dma_start(out=x_sb[:, i, :], in_=x_rows[P * i : P * i + P, :])
+            wb_sb = front.tile([P, B_TILES, ROW_SLOT], BF16)
+            wb_rows = wkv_b_w.rearrange("(n p) c -> p n c", p=P)
+            for c in range(B_CHUNKS):
+                nc.sync.dma_start(
+                    out=wb_sb[:, 4 * c : 4 * c + 4, 1 : 1 + KV_RANK + 1], in_=wb_rows[:, 4 * c : 4 * c + 4, :]
                 )
+            cos_sb = front.tile([P, 2, ROPE // 2], BF16)
+            nc.sync.dma_start(out=cos_sb[:], in_=freqs_cos.rearrange("(h p) j -> p h j", p=P))
+            sin_sb = front.tile([P, 2, ROPE // 2], BF16)
+            nc.sync.dma_start(out=sin_sb[:], in_=freqs_sin.rearrange("(h p) j -> p h j", p=P))
+            nc.sync.dma_start(out=bias_b[:].rearrange("p h f -> p (h f)"), in_=wkv_b_b.partition_broadcast(P))
 
-        x_codes = const.tile([P, TOKEN_TILES, PASSES_A * P], U32, align_bytes=64)
-        x_scales = const.tile([P, TOKEN_TILES, PASSES_A * P], U8, align_bytes=64)
-        sp_codes = const.tile([P, TOKEN_TILES, P], U32, align_bytes=64)
-        sp_scales = const.tile([P, TOKEN_TILES, P], U8, align_bytes=64)
-        x_rows = x.rearrange("b s k -> (b s) k")
-        for i in range(TOKEN_TILES):
-            grouped = regroup(load_rows(x_rows[P * i : P * i + P, :]))
-            nc.vector.quantize_mx(
-                out=x_codes[:, i, :].bitcast(FP8X4),
-                scales=x_scales[:, i, :],
-                in_=grouped[:].rearrange("p g r u -> p (g r u)").bitcast(BF16),
-            )
-
-        kv_all = const.tile([P, TOKEN_TILES, KV_RANK], F32)
-        pe_all = const.tile([P, TOKEN_TILES, ROPE], F32)
-        gained = const.tile([P, TOKEN_TILES, KV_RANK], F32)
-        junk_kv = const.tile([P, 2, KV_RANK], BF16)
-        junk_gained = const.tile([P, 2, KV_RANK], BF16)
-        sum_kv2 = const.tile([P, TOKEN_TILES], F32)
-        sum_gained2 = const.tile([P, TOKEN_TILES], F32)
-        pe_ps = pe_psum.tile([P, TOKEN_TILES, ROPE], F32)
-        for i in range(TOKEN_TILES):
-            kv_ps = acc_psum.tile([P, BANK], F32, tag="acc")
-            for out_ps, cols in ((kv_ps[:], slice(0, KV_RANK)), (pe_ps[:, i, :], slice(KV_RANK, A_OUT))):
-                for g in range(PASSES_A):
-                    nc.tensor.matmul_mx(
-                        out=out_ps,
-                        lhsT=x_codes[:, i, P * g : P * g + P].bitcast(FP8X4),
-                        lhsT_scale=x_scales[:, i, P * g : P * g + P],
-                        rhs=wa_codes[:, g, cols].bitcast(FP8X4),
-                        rhs_scale=wa_scales[:, g, cols],
-                        start=(g == 0),
-                        stop=(g == PASSES_A - 1),
+            def spread_rows(first_row, n_rows):
+                spread = turn_psum.tile([P, 2 * BANK], BF16, tag="turned")
+                for r in range(n_rows):
+                    nc.tensor.matmul(
+                        out=spread[:, P * r : P * r + P],
+                        lhsT=ident_bf[:, first_row + r : first_row + r + 1].to_broadcast([P, P]),
+                        rhs=vec_rows[:],
+                        start=True,
+                        stop=True,
                     )
-            nc.vector.tensor_tensor(out=kv_all[:, i, :], in0=kv_ps[:], in1=bias_a[:, 0:KV_RANK], op=ALU.add)
-            nc.scalar.activation(
-                out=junk_kv[:, i % 2, :], in_=kv_all[:, i, :], func=ACT.Square, accum_out=sum_kv2[:, i : i + 1]
-            )
-            nc.vector.tensor_tensor(out=gained[:, i, :], in0=kv_all[:, i, :], in1=gain[:], op=ALU.mult)
-            nc.scalar.activation(
-                out=junk_gained[:, i % 2, :],
-                in_=gained[:, i, :],
-                func=ACT.Square,
-                accum_out=sum_gained2[:, i : i + 1],
-            )
-        nc.vector.tensor_tensor(
-            out=pe_all[:],
-            in0=pe_ps[:],
-            in1=bias_a[:, KV_RANK:A_OUT].unsqueeze(1).to_broadcast([P, TOKEN_TILES, ROPE]),
-            op=ALU.add,
-        )
+                return spread
 
-        rms = const.tile([P, TOKEN_TILES], F32)
-        nc.scalar.activation(out=rms[:], in_=sum_kv2[:], func=ACT.Sqrt, bias=eps_col[:], scale=1.0 / KV_RANK)
-        inv_rms = const.tile([P, TOKEN_TILES], F32)
-        nc.vector.reciprocal(out=inv_rms[:], in_=rms[:])
-        sp_bf = const.tile([P, TOKEN_TILES, KV_RANK], BF16)
-        for i in range(TOKEN_TILES):
-            nc.vector.tensor_scalar(
-                out=sp_bf[:, i, :], in0=gained[:, i, :], scalar1=inv_rms[:, i : i + 1], scalar2=None, op0=ALU.mult
-            )
-        sum_sp2 = const.tile([P, TOKEN_TILES], F32)
-        nc.vector.tensor_tensor(out=sum_sp2[:], in0=sum_gained2[:], in1=inv_rms[:], op=ALU.mult)
-        nc.vector.tensor_tensor(out=sum_sp2[:], in0=sum_sp2[:], in1=inv_rms[:], op=ALU.mult)
-        time_t = const.tile([P, TOKEN_TILES], F32)
-        nc.scalar.activation(out=time_t[:], in_=sum_sp2[:], func=ACT.Sqrt, bias=one_col[:], scale=1.0)
-
-        sp_grouped = const.tile([P, TOKEN_TILES, P, 4], BF16, align_bytes=64)
-        for pair in range(TOKEN_TILES // 2):
-            sp_turned = turn_psum.tile([P, 2, 4, P], BF16, tag="turned")
-            for i2 in range(2):
-                for t in range(4):
-                    nc.tensor.transpose(
-                        sp_turned[:, i2, t, :], sp_bf[:, 2 * pair + i2, P * t : P * t + P], ident_bf[:]
-                    )
+            bias_a = front.tile([P, A_OUT], BF16)
+            spread_a = spread_rows(A_ROW0, A_TILES)
             nc.vector.tensor_copy(
-                out=sp_grouped[:, 2 * pair : 2 * pair + 2], in_=sp_turned[:].rearrange("p i t r -> p i r t")
+                out=bias_a[:, 0:KV_RANK].rearrange("p (u e q) -> p u e q", u=2, e=2),
+                in_=spread_a[:, 0:KV_RANK].rearrange("p (u q e) -> p u e q", u=2, e=2),
             )
-        nc.vector.quantize_mx(
-            out=sp_codes[:].rearrange("p i r -> p (i r)").bitcast(FP8X4),
-            scales=sp_scales[:].rearrange("p i r -> p (i r)"),
-            in_=sp_grouped[:].rearrange("p i r t -> p (i r t)"),
-        )
+            nc.vector.tensor_copy(out=bias_a[:, KV_RANK:A_OUT], in_=spread_a[:, KV_RANK:A_OUT])
+            gain = front.tile([P, KV_RANK], BF16)
+            spread_g = spread_rows(G_ROW0, KV_RANK // P)
+            nc.vector.tensor_copy(
+                out=gain[:].rearrange("p (u e q) -> p u e q", u=2, e=2),
+                in_=spread_g[:, 0:KV_RANK].rearrange("p (u q e) -> p u e q", u=2, e=2),
+            )
 
-        HALF = ROPE // 2
-        pe_pairs = pe_all[:].rearrange("p i (j two) -> p (i j) two", two=2)
-        even = pe_pairs[:, :, 0].rearrange("p (b hj) -> p b hj", b=2)
-        odd = pe_pairs[:, :, 1].rearrange("p (b hj) -> p b hj", b=2)
-        cos = cos_sb[:].rearrange("p h j -> p (h j)").unsqueeze(1).to_broadcast([P, 2, 2 * HALF])
-        sin = sin_sb[:].rearrange("p h j -> p (h j)").unsqueeze(1).to_broadcast([P, 2, 2 * HALF])
-        even_cos = const.tile([P, 2, 2 * HALF], F32)
-        nc.gpsimd.tensor_tensor(out=even_cos[:], in0=even, in1=cos, op=ALU.mult)
-        odd_sin = const.tile([P, 2, 2 * HALF], F32)
-        nc.gpsimd.tensor_tensor(out=odd_sin[:], in0=odd, in1=sin, op=ALU.mult)
-        even_sin = const.tile([P, 2, 2 * HALF], F32)
-        nc.gpsimd.tensor_tensor(out=even_sin[:], in0=even, in1=sin, op=ALU.mult)
-        odd_cos = const.tile([P, 2, 2 * HALF], F32)
-        nc.gpsimd.tensor_tensor(out=odd_cos[:], in0=odd, in1=cos, op=ALU.mult)
-        k_pe = const.tile([P, TOKEN_TILES, ROPE], F32)
-        k_pe_pairs = k_pe[:].rearrange("p i (j two) -> p (i j) two", two=2)
-        nc.gpsimd.tensor_tensor(
-            out=k_pe_pairs[:, :, 0],
-            in0=even_cos[:].rearrange("p b hj -> p (b hj)"),
-            in1=odd_sin[:].rearrange("p b hj -> p (b hj)"),
-            op=ALU.subtract,
-        )
-        nc.gpsimd.tensor_tensor(
-            out=k_pe_pairs[:, :, 1],
-            in0=even_sin[:].rearrange("p b hj -> p (b hj)"),
-            in1=odd_cos[:].rearrange("p b hj -> p (b hj)"),
-            op=ALU.add,
-        )
-        k_outs = []
-        junk_pe = const.tile([P, 2, ROPE], BF16)
-        sum_pe2 = const.tile([P, TOKEN_TILES], F32)
-        for i in range(TOKEN_TILES):
-            k_out = outs.tile([P, HEADS, 1 + NOPE + ROPE], F32)
-            k_outs.append(k_out)
-            nc.gpsimd.tensor_scalar(
-                out=k_out[:, :, 1 + NOPE :],
-                in0=k_pe[:, i, :].unsqueeze(1).to_broadcast([P, HEADS, ROPE]),
-                scalar1=1.0,
-                scalar2=0.0,
-                op0=ALU.mult,
-                op1=ALU.add,
-            )
-            nc.scalar.activation(
-                out=junk_pe[:, i % 2, :],
-                in_=k_out[:, 0, 1 + NOPE :],
-                func=ACT.Square,
-                accum_out=sum_pe2[:, i : i + 1],
-            )
-        pe_norm = const.tile([P, TOKEN_TILES], F32)
-        nc.gpsimd.tensor_scalar(out=pe_norm[:], in0=sum_pe2[:], scalar1=1.0, scalar2=1.0, op0=ALU.mult, op1=ALU.add)
-
-        wb_codes = const.tile([P, B_OUT], U32, align_bytes=64)
-        wb_scales = const.tile([P, B_OUT], U8, align_bytes=64)
-        w0_all = const.tile([P, B_OUT], BF16)
-        by_head = wkv_b_w.rearrange("(h f) c -> f h c", f=HEAD_ROWS)
-        for c in range(B_CHUNKS):
-            chunk = chunk_pool.tile([P, 4, ROW_SLOT], BF16)
-            if c < K_CHUNKS:
-                for two in range(2):
-                    nc.sync.dma_start(
-                        out=chunk[NOPE * two : NOPE * (two + 1), :, 1 : 1 + KV_RANK + 1],
-                        in_=by_head[0:NOPE, 8 * c + two : 8 * (c + 1) : 2, :],
+            wa_words = wa_sb[:].bitcast(F32)
+            for j in range(A_TILES):
+                grouped = regroup([wa_words[:, j, WORDS * g : WORDS * (g + 1)] for g in range(PASSES_A)])
+                for g in range(PASSES_A):
+                    nc.vector.quantize_mx(
+                        out=wa_codes[:, g, P * j : P * j + P].bitcast(FP8X4),
+                        scales=wa_scales[:, g, P * j : P * j + P],
+                        in_=grouped[:, g].rearrange("p r u -> p (r u)").bitcast(BF16),
                     )
-            else:
-                h0 = 4 * (c - K_CHUNKS)
-                nc.sync.dma_start(out=chunk[:, :, 1 : 1 + KV_RANK + 1], in_=by_head[NOPE:HEAD_ROWS, h0 : h0 + 4, :])
-            words = chunk[:].bitcast(F32)
-            grouped = regroup([words[:, m, 1 : 1 + WORDS] for m in range(4)])
-            cols = slice(BANK * c, BANK * (c + 1))
-            nc.vector.quantize_mx(
-                out=wb_codes[:, cols].bitcast(FP8X4),
-                scales=wb_scales[:, cols],
-                in_=grouped[:].rearrange("p m r u -> p (m r u)").bitcast(BF16),
-            )
-            w0_ps = turn_psum.tile([P, BANK], BF16, tag="turned")
-            for m in range(4):
-                nc.tensor.matmul(
-                    out=w0_ps[:, P * m : P * m + P],
-                    lhsT=chunk[:, m, 1:2].to_broadcast([P, P]),
-                    rhs=ident_bf[:],
-                    start=True,
-                    stop=True,
+            x_words = x_sb[:].bitcast(F32)
+            for i in range(TOKEN_TILES):
+                grouped = regroup([x_words[:, i, WORDS * g : WORDS * (g + 1)] for g in range(PASSES_A)])
+                nc.vector.quantize_mx(
+                    out=x_codes[:, i, :].bitcast(FP8X4),
+                    scales=x_scales[:, i, :],
+                    in_=grouped[:].rearrange("p g r u -> p (g r u)").bitcast(BF16),
                 )
-            nc.vector.tensor_copy(out=w0_all[:, cols], in_=w0_ps[:])
 
-        k_rows = out_0.rearrange("b s h c -> (b s) (h c)")
-        v_rows = out_1.rearrange("b s h c -> (b s) (h c)")
-        for i in range(TOKEN_TILES):
-            k_out = k_outs[i]
-            v_out = outs.tile([P, HEADS, 1 + V_DIM], F32, bufs=2)
-            k_part = work.tile([P, HEADS, NOPE], F32)
+            kv_all = front.tile([P, TOKEN_TILES, KV_RANK], F32)
+            pe_all = front.tile([P, TOKEN_TILES, ROPE], F32)
+            gained = front.tile([P, TOKEN_TILES, KV_RANK], F32)
+            junk_kv = front.tile([P, 2, KV_RANK], BF16)
+            junk_gained = front.tile([P, 2, KV_RANK], BF16)
+            sum_kv2 = front.tile([P, TOKEN_TILES], F32)
+            sum_gained2 = front.tile([P, TOKEN_TILES], F32)
+            pe_ps = pe_psum.tile([P, TOKEN_TILES, ROPE], F32)
+            for i in range(TOKEN_TILES):
+                kv_ps = acc_psum.tile([P, BANK], F32, tag="acc")
+                for out_ps, cols in ((kv_ps[:], slice(0, KV_RANK)), (pe_ps[:, i, :], slice(KV_RANK, A_OUT))):
+                    for g in range(PASSES_A):
+                        nc.tensor.matmul_mx(
+                            out=out_ps,
+                            lhsT=x_codes[:, i, P * g : P * g + P].bitcast(FP8X4),
+                            lhsT_scale=x_scales[:, i, P * g : P * g + P],
+                            rhs=wa_codes[:, g, cols].bitcast(FP8X4),
+                            rhs_scale=wa_scales[:, g, cols],
+                            start=(g == 0),
+                            stop=(g == PASSES_A - 1),
+                        )
+                nc.vector.tensor_tensor(out=kv_all[:, i, :], in0=kv_ps[:], in1=bias_a[:, 0:KV_RANK], op=ALU.add)
+                nc.scalar.activation(
+                    out=junk_kv[:, i % 2, :], in_=kv_all[:, i, :], func=ACT.Square, accum_out=sum_kv2[:, i : i + 1]
+                )
+                nc.vector.tensor_tensor(out=gained[:, i, :], in0=kv_all[:, i, :], in1=gain[:], op=ALU.mult)
+                nc.scalar.activation(
+                    out=junk_gained[:, i % 2, :],
+                    in_=gained[:, i, :],
+                    func=ACT.Square,
+                    accum_out=sum_gained2[:, i : i + 1],
+                )
+            nc.vector.tensor_tensor(
+                out=pe_all[:],
+                in0=pe_ps[:],
+                in1=bias_a[:, KV_RANK:A_OUT].unsqueeze(1).to_broadcast([P, TOKEN_TILES, ROPE]),
+                op=ALU.add,
+            )
+
+            rms = front.tile([P, TOKEN_TILES], F32)
+            nc.scalar.activation(out=rms[:], in_=sum_kv2[:], func=ACT.Sqrt, bias=eps_col[:], scale=1.0 / KV_RANK)
+            inv_rms = front.tile([P, TOKEN_TILES], F32)
+            nc.vector.reciprocal(out=inv_rms[:], in_=rms[:])
+            sp_bf = front.tile([P, TOKEN_TILES, KV_RANK], BF16)
+            for i in range(TOKEN_TILES):
+                nc.vector.tensor_scalar(
+                    out=sp_bf[:, i, :], in0=gained[:, i, :], scalar1=inv_rms[:, i : i + 1], scalar2=None, op0=ALU.mult
+                )
+            sum_sp2 = front.tile([P, TOKEN_TILES], F32)
+            nc.vector.tensor_tensor(out=sum_sp2[:], in0=sum_gained2[:], in1=inv_rms[:], op=ALU.mult)
+            nc.vector.tensor_tensor(out=sum_sp2[:], in0=sum_sp2[:], in1=inv_rms[:], op=ALU.mult)
+            nc.scalar.activation(out=time_t[:], in_=sum_sp2[:], func=ACT.Sqrt, bias=one_col[:], scale=1.0)
+
+            sp_grouped = front.tile([P, TOKEN_TILES, P, 4], BF16, align_bytes=64)
+            for pair in range(TOKEN_TILES // 2):
+                sp_turned = turn_psum.tile([P, 2, 4, P], BF16, tag="turned")
+                for i2 in range(2):
+                    for t in range(4):
+                        nc.tensor.transpose(
+                            sp_turned[:, i2, t, :], sp_bf[:, 2 * pair + i2, P * t : P * t + P], ident_bf[:]
+                        )
+                nc.vector.tensor_copy(
+                    out=sp_grouped[:, 2 * pair : 2 * pair + 2], in_=sp_turned[:].rearrange("p i t r -> p i r t")
+                )
+            nc.vector.quantize_mx(
+                out=sp_codes[:].rearrange("p i r -> p (i r)").bitcast(FP8X4),
+                scales=sp_scales[:].rearrange("p i r -> p (i r)"),
+                in_=sp_grouped[:].rearrange("p i r t -> p (i r t)"),
+            )
+
+            pe_pairs = pe_all[:].rearrange("p i (j two) -> p (i j) two", two=2)
+            even = pe_pairs[:, :, 0].rearrange("p (b hj) -> p b hj", b=2)
+            odd = pe_pairs[:, :, 1].rearrange("p (b hj) -> p b hj", b=2)
+            cos = cos_sb[:].rearrange("p h j -> p (h j)").unsqueeze(1).to_broadcast([P, 2, ROPE])
+            sin = sin_sb[:].rearrange("p h j -> p (h j)").unsqueeze(1).to_broadcast([P, 2, ROPE])
+            even_cos = front.tile([P, 2, ROPE], F32)
+            nc.gpsimd.tensor_tensor(out=even_cos[:], in0=even, in1=cos, op=ALU.mult)
+            odd_sin = front.tile([P, 2, ROPE], F32)
+            nc.gpsimd.tensor_tensor(out=odd_sin[:], in0=odd, in1=sin, op=ALU.mult)
+            even_sin = front.tile([P, 2, ROPE], F32)
+            nc.gpsimd.tensor_tensor(out=even_sin[:], in0=even, in1=sin, op=ALU.mult)
+            odd_cos = front.tile([P, 2, ROPE], F32)
+            nc.gpsimd.tensor_tensor(out=odd_cos[:], in0=odd, in1=cos, op=ALU.mult)
+            k_pe_pairs = k_pe[:].rearrange("p i (j two) -> p (i j) two", two=2)
+            nc.gpsimd.tensor_tensor(
+                out=k_pe_pairs[:, :, 0],
+                in0=even_cos[:].rearrange("p b hj -> p (b hj)"),
+                in1=odd_sin[:].rearrange("p b hj -> p (b hj)"),
+                op=ALU.subtract,
+            )
+            nc.gpsimd.tensor_tensor(
+                out=k_pe_pairs[:, :, 1],
+                in0=even_sin[:].rearrange("p b hj -> p (b hj)"),
+                in1=odd_cos[:].rearrange("p b hj -> p (b hj)"),
+                op=ALU.add,
+            )
+
+            wb_words = wb_sb[:].bitcast(F32)
             for c in range(B_CHUNKS):
                 cols = slice(BANK * c, BANK * (c + 1))
-                y_ps = acc_psum.tile([P, BANK], F32, tag="acc")
-                nc.tensor.matmul_mx(
-                    out=y_ps[:],
-                    lhsT=sp_codes[:, i, :].bitcast(FP8X4),
-                    lhsT_scale=sp_scales[:, i, :],
-                    rhs=wb_codes[:, cols].bitcast(FP8X4),
-                    rhs_scale=wb_scales[:, cols],
-                    start=True,
-                    stop=True,
+                grouped = regroup([wb_words[:, 4 * c + m, 1 : 1 + WORDS] for m in range(4)])
+                nc.vector.quantize_mx(
+                    out=wb_codes[:, cols].bitcast(FP8X4),
+                    scales=wb_scales[:, cols],
+                    in_=grouped[:].rearrange("p m r u -> p (m r u)").bitcast(BF16),
                 )
-                if c < K_CHUNKS:
-                    dest = k_part[:, 8 * c : 8 * (c + 1), :]
-                    width = NOPE
-                else:
-                    h0 = 4 * (c - K_CHUNKS)
-                    dest = v_out[:, h0 : h0 + 4, 1:]
-                    width = V_DIM
-                nc.vector.scalar_tensor_tensor(
-                    out=dest,
-                    in0=w0_all[:, cols].rearrange("p (h f) -> p h f", f=width),
-                    scalar=time_t[:, i : i + 1],
-                    in1=y_ps[:].rearrange("p (h f) -> p h f", f=width),
+                w0_ps = turn_psum.tile([P, BANK], BF16, tag="turned")
+                for m in range(4):
+                    nc.tensor.matmul(
+                        out=w0_ps[:, P * m : P * m + P],
+                        lhsT=wb_sb[:, 4 * c + m, 1:2].to_broadcast([P, P]),
+                        rhs=ident_bf[:],
+                        start=True,
+                        stop=True,
+                    )
+                nc.vector.tensor_copy(out=w0_all[:, cols], in_=w0_ps[:])
+
+        with tc.tile_pool(name="back", bufs=2) as back:
+            k_rows = out_0.rearrange("b s h c -> (b s) (h c)")
+            v_rows = out_1.rearrange("b s h c -> (b s) (h c)")
+            junk_head = back.tile([P, 4, V_DIM], BF16, bufs=1)
+            for i in range(TOKEN_TILES):
+                k_out = back.tile([P, HEADS, 1 + NOPE + ROPE], F32)
+                v_out = back.tile([P, HEADS, 1 + V_DIM], F32)
+                nc.gpsimd.tensor_scalar(
+                    out=k_out[:, :, 1 + NOPE :],
+                    in0=k_pe[:, i, :].unsqueeze(1).to_broadcast([P, HEADS, ROPE]),
+                    scalar1=1.0,
+                    scalar2=0.0,
                     op0=ALU.mult,
                     op1=ALU.add,
                 )
-            nc.gpsimd.tensor_tensor(out=k_out[:, :, 1 : 1 + NOPE], in0=k_part[:], in1=bias_b[:, :, 0:NOPE], op=ALU.add)
-            for h0 in range(0, HEADS, 4):
-                nc.vector.tensor_tensor(
-                    out=v_out[:, h0 : h0 + 4, 1:],
-                    in0=v_out[:, h0 : h0 + 4, 1:],
-                    in1=bias_b[:, h0 : h0 + 4, NOPE:],
-                    op=ALU.add,
+                sum_pe2 = back.tile([P, 1], F32)
+                nc.scalar.activation(
+                    out=junk_head[:, 0, :], in_=k_out[:, 0, 1 + NOPE :], func=ACT.Square, accum_out=sum_pe2[:]
                 )
-            sum_k2 = small.tile([P, HEADS], F32)
-            sum_v2 = small.tile([P, HEADS], F32)
-            v_squares = work.tile([P, HEADS, V_DIM], F32, bufs=1)
-            for h0 in range(0, HEADS, 4):
-                nc.scalar.activation(out=v_squares[:, h0 : h0 + 4, :], in_=v_out[:, h0 : h0 + 4, 1:], func=ACT.Square)
-            nc.vector.tensor_reduce(out=sum_v2[:], in_=v_squares[:], axis=mybir.AxisListType.X, op=ALU.add)
-            nc.scalar.activation(out=v_out[:, :, 0], in_=sum_v2[:], func=ACT.Sqrt, bias=one_col[:], scale=1.0)
-            nc.sync.dma_start(out=v_rows[P * i : P * i + P, :], in_=v_out[:].rearrange("p h c -> p (h c)"))
-            k_squares = work.tile([P, HEADS, NOPE], F32, bufs=1)
-            nc.scalar.activation(out=k_squares[:], in_=k_out[:, :, 1 : 1 + NOPE], func=ACT.Square)
-            nc.vector.tensor_reduce(out=sum_k2[:], in_=k_squares[:], axis=mybir.AxisListType.X, op=ALU.add)
-            nc.scalar.activation(out=k_out[:, :, 0], in_=sum_k2[:], func=ACT.Sqrt, bias=pe_norm[:, i : i + 1], scale=1.0)
-            nc.sync.dma_start(out=k_rows[P * i : P * i + P, :], in_=k_out[:].rearrange("p h c -> p (h c)"))
+                pe_norm = back.tile([P, 1], F32)
+                nc.gpsimd.tensor_scalar(
+                    out=pe_norm[:], in0=sum_pe2[:], scalar1=1.0, scalar2=1.0, op0=ALU.mult, op1=ALU.add
+                )
+                y = back.tile([P, HEADS, HEAD_ROWS], F32)
+                y_flat = y[:].rearrange("p h f -> p (h f)")
+                for c in range(B_CHUNKS):
+                    cols = slice(BANK * c, BANK * (c + 1))
+                    y_ps = acc_psum.tile([P, BANK], F32, tag="acc")
+                    nc.tensor.matmul_mx(
+                        out=y_ps[:],
+                        lhsT=sp_codes[:, i, :].bitcast(FP8X4),
+                        lhsT_scale=sp_scales[:, i, :],
+                        rhs=wb_codes[:, cols].bitcast(FP8X4),
+                        rhs_scale=wb_scales[:, cols],
+                        start=True,
+                        stop=True,
+                    )
+                    nc.vector.scalar_tensor_tensor(
+                        out=y_flat[:, cols],
+                        in0=w0_all[:, cols],
+                        scalar=time_t[:, i : i + 1],
+                        in1=y_ps[:],
+                        op0=ALU.mult,
+                        op1=ALU.add,
+                    )
+                sum_k2 = back.tile([P, HEADS], F32)
+                sum_v2 = back.tile([P, HEADS], F32)
+                for heads in (slice(0, HEADS // 2), slice(HEADS // 2, HEADS)):
+                    nc.gpsimd.tensor_tensor(
+                        out=k_out[:, heads, 1 : 1 + NOPE], in0=y[:, heads, 0:NOPE], in1=bias_b[:, heads, 0:NOPE], op=ALU.add
+                    )
+                    nc.vector.tensor_tensor(
+                        out=v_out[:, heads, 1:], in0=y[:, heads, NOPE:], in1=bias_b[:, heads, NOPE:], op=ALU.add
+                    )
+                for h in range(HEADS):
+                    nc.scalar.activation(
+                        out=junk_head[:, h % 4, :],
+                        in_=v_out[:, h, 1:],
+                        func=ACT.Square,
+                        accum_out=sum_v2[:, h : h + 1],
+                    )
+                nc.scalar.activation(out=v_out[:, :, 0], in_=sum_v2[:], func=ACT.Sqrt, bias=one_col[:], scale=1.0)
+                nc.sync.dma_start(out=v_rows[P * i : P * i + P, :], in_=v_out[:].rearrange("p h c -> p (h c)"))
+                for h in range(HEADS):
+                    nc.scalar.activation(
+                        out=junk_head[:, h % 4, 0:NOPE],
+                        in_=k_out[:, h, 1 : 1 + NOPE],
+                        func=ACT.Square,
+                        accum_out=sum_k2[:, h : h + 1],
+                    )
+                nc.scalar.activation(out=k_out[:, :, 0], in_=sum_k2[:], func=ACT.Sqrt, bias=pe_norm[:], scale=1.0)
+                nc.sync.dma_start(out=k_rows[P * i : P * i + P, :], in_=k_out[:].rearrange("p h c -> p (h c)"))

@@ -43,9 +43,11 @@ def tile_lorentzmla_pa_kernel(
     nc = tc.nc
     with ExitStack() as ctx:
         keep = ctx.enter_context(tc.tile_pool(name="keep", bufs=1))
+        front = ctx.enter_context(tc.tile_pool(name="front", bufs=1))
         stage = ctx.enter_context(tc.tile_pool(name="stage", bufs=3))
-        turn_psum = ctx.enter_context(tc.psum_pool(name="turn_psum", bufs=3))
-        acc_psum = ctx.enter_context(tc.psum_pool(name="acc_psum", bufs=4))
+        back = ctx.enter_context(tc.tile_pool(name="back", bufs=2))
+        turn_psum = ctx.enter_context(tc.psum_pool(name="turn_psum", bufs=4))
+        acc_psum = ctx.enter_context(tc.psum_pool(name="acc_psum", bufs=3))
         pe_psum = ctx.enter_context(tc.psum_pool(name="pe_psum", bufs=1))
 
         wa_codes = keep.tile([P, PASSES_A, A_OUT], U32, align_bytes=64)
@@ -86,224 +88,228 @@ def tile_lorentzmla_pa_kernel(
                 )
             return grouped
 
-        with tc.tile_pool(name="front", bufs=1) as front:
-            A_ROW0, G_ROW0 = 0, 32
-            vec_rows = front.tile([P, P], BF16)
-            nc.vector.memset(vec_rows[:], 0.0)
+        A_ROW0, G_ROW0 = 0, 32
+        vec_rows = front.tile([P, P], BF16)
+        nc.vector.memset(vec_rows[:], 0.0)
+        nc.sync.dma_start(
+            out=vec_rows[A_ROW0 : A_ROW0 + A_TILES, :], in_=wkv_a_b.rearrange("(r c) -> r c", c=P)
+        )
+        nc.sync.dma_start(
+            out=vec_rows[G_ROW0 : G_ROW0 + KV_RANK // P, :], in_=kv_norm_w.rearrange("(r c) -> r c", c=P)
+        )
+        wa_sb = front.tile([P, A_TILES, DIM], BF16)
+        kv_rows = wkv_a_w[0:KV_RANK, :].rearrange("(u q e) k -> u e q k", u=2, e=2)
+        for j in range(KV_RANK // P):
+            nc.sync.dma_start(out=wa_sb[:, j, :], in_=kv_rows[j // 2, j % 2])
+        nc.sync.dma_start(out=wa_sb[:, KV_RANK // P, :], in_=wkv_a_w[KV_RANK:A_OUT, :])
+        x_sb = front.tile([P, TOKEN_TILES, DIM], BF16)
+        x_rows = x.rearrange("b s k -> (b s) k")
+        for i in range(TOKEN_TILES):
+            nc.sync.dma_start(out=x_sb[:, i, :], in_=x_rows[P * i : P * i + P, :])
+        wb_sb = front.tile([P, B_TILES, ROW_SLOT], BF16)
+        wb_rows = wkv_b_w.rearrange("(n p) c -> p n c", p=P)
+        for c in range(B_CHUNKS):
             nc.sync.dma_start(
-                out=vec_rows[A_ROW0 : A_ROW0 + A_TILES, :], in_=wkv_a_b.rearrange("(r c) -> r c", c=P)
+                out=wb_sb[:, 4 * c : 4 * c + 4, 1 : 1 + KV_RANK + 1], in_=wb_rows[:, 4 * c : 4 * c + 4, :]
             )
-            nc.sync.dma_start(
-                out=vec_rows[G_ROW0 : G_ROW0 + KV_RANK // P, :], in_=kv_norm_w.rearrange("(r c) -> r c", c=P)
-            )
-            wa_sb = front.tile([P, A_TILES, DIM], BF16)
-            kv_rows = wkv_a_w[0:KV_RANK, :].rearrange("(u q e) k -> u e q k", u=2, e=2)
-            for j in range(KV_RANK // P):
-                nc.sync.dma_start(out=wa_sb[:, j, :], in_=kv_rows[j // 2, j % 2])
-            nc.sync.dma_start(out=wa_sb[:, KV_RANK // P, :], in_=wkv_a_w[KV_RANK:A_OUT, :])
-            x_sb = front.tile([P, TOKEN_TILES, DIM], BF16)
-            x_rows = x.rearrange("b s k -> (b s) k")
-            for i in range(TOKEN_TILES):
-                nc.sync.dma_start(out=x_sb[:, i, :], in_=x_rows[P * i : P * i + P, :])
-            wb_sb = front.tile([P, B_TILES, ROW_SLOT], BF16)
-            wb_rows = wkv_b_w.rearrange("(n p) c -> p n c", p=P)
-            for c in range(B_CHUNKS):
-                nc.sync.dma_start(
-                    out=wb_sb[:, 4 * c : 4 * c + 4, 1 : 1 + KV_RANK + 1], in_=wb_rows[:, 4 * c : 4 * c + 4, :]
+        cos_sb = front.tile([P, 2, ROPE // 2], BF16)
+        nc.sync.dma_start(out=cos_sb[:], in_=freqs_cos.rearrange("(h p) j -> p h j", p=P))
+        sin_sb = front.tile([P, 2, ROPE // 2], BF16)
+        nc.sync.dma_start(out=sin_sb[:], in_=freqs_sin.rearrange("(h p) j -> p h j", p=P))
+        nc.sync.dma_start(out=bias_b[:].rearrange("p h f -> p (h f)"), in_=wkv_b_b.partition_broadcast(P))
+
+        def spread_rows(first_row, n_rows):
+            spread = turn_psum.tile([P, 2 * BANK], BF16, tag="turned")
+            for r in range(n_rows):
+                nc.tensor.matmul(
+                    out=spread[:, P * r : P * r + P],
+                    lhsT=ident_bf[:, first_row + r : first_row + r + 1].to_broadcast([P, P]),
+                    rhs=vec_rows[:],
+                    start=True,
+                    stop=True,
                 )
-            cos_sb = front.tile([P, 2, ROPE // 2], BF16)
-            nc.sync.dma_start(out=cos_sb[:], in_=freqs_cos.rearrange("(h p) j -> p h j", p=P))
-            sin_sb = front.tile([P, 2, ROPE // 2], BF16)
-            nc.sync.dma_start(out=sin_sb[:], in_=freqs_sin.rearrange("(h p) j -> p h j", p=P))
-            nc.sync.dma_start(out=bias_b[:].rearrange("p h f -> p (h f)"), in_=wkv_b_b.partition_broadcast(P))
+            return spread
 
-            def spread_rows(first_row, n_rows):
-                spread = turn_psum.tile([P, 2 * BANK], BF16, tag="turned")
-                for r in range(n_rows):
-                    nc.tensor.matmul(
-                        out=spread[:, P * r : P * r + P],
-                        lhsT=ident_bf[:, first_row + r : first_row + r + 1].to_broadcast([P, P]),
-                        rhs=vec_rows[:],
-                        start=True,
-                        stop=True,
-                    )
-                return spread
+        bias_a = front.tile([P, A_OUT], BF16)
+        spread_a = spread_rows(A_ROW0, A_TILES)
+        nc.vector.tensor_copy(
+            out=bias_a[:, 0:KV_RANK].rearrange("p (u e q) -> p u e q", u=2, e=2),
+            in_=spread_a[:, 0:KV_RANK].rearrange("p (u q e) -> p u e q", u=2, e=2),
+        )
+        nc.vector.tensor_copy(out=bias_a[:, KV_RANK:A_OUT], in_=spread_a[:, KV_RANK:A_OUT])
+        gain = front.tile([P, KV_RANK], BF16)
+        spread_g = spread_rows(G_ROW0, KV_RANK // P)
+        nc.vector.tensor_copy(
+            out=gain[:].rearrange("p (u e q) -> p u e q", u=2, e=2),
+            in_=spread_g[:, 0:KV_RANK].rearrange("p (u q e) -> p u e q", u=2, e=2),
+        )
 
-            bias_a = front.tile([P, A_OUT], BF16)
-            spread_a = spread_rows(A_ROW0, A_TILES)
-            nc.vector.tensor_copy(
-                out=bias_a[:, 0:KV_RANK].rearrange("p (u e q) -> p u e q", u=2, e=2),
-                in_=spread_a[:, 0:KV_RANK].rearrange("p (u q e) -> p u e q", u=2, e=2),
-            )
-            nc.vector.tensor_copy(out=bias_a[:, KV_RANK:A_OUT], in_=spread_a[:, KV_RANK:A_OUT])
-            gain = front.tile([P, KV_RANK], BF16)
-            spread_g = spread_rows(G_ROW0, KV_RANK // P)
-            nc.vector.tensor_copy(
-                out=gain[:].rearrange("p (u e q) -> p u e q", u=2, e=2),
-                in_=spread_g[:, 0:KV_RANK].rearrange("p (u q e) -> p u e q", u=2, e=2),
-            )
-
-            wa_words = wa_sb[:].bitcast(F32)
-            for j in range(A_TILES):
-                grouped = regroup([wa_words[:, j, WORDS * g : WORDS * (g + 1)] for g in range(PASSES_A)])
-                for g in range(PASSES_A):
-                    nc.vector.quantize_mx(
-                        out=wa_codes[:, g, P * j : P * j + P].bitcast(FP8X4),
-                        scales=wa_scales[:, g, P * j : P * j + P],
-                        in_=grouped[:, g].rearrange("p r u -> p (r u)").bitcast(BF16),
-                    )
-            x_words = x_sb[:].bitcast(F32)
-            for i in range(TOKEN_TILES):
-                grouped = regroup([x_words[:, i, WORDS * g : WORDS * (g + 1)] for g in range(PASSES_A)])
+        wa_words = wa_sb[:].bitcast(F32)
+        for j in range(A_TILES):
+            grouped = regroup([wa_words[:, j, WORDS * g : WORDS * (g + 1)] for g in range(PASSES_A)])
+            for g in range(PASSES_A):
                 nc.vector.quantize_mx(
-                    out=x_codes[:, i, :].bitcast(FP8X4),
-                    scales=x_scales[:, i, :],
-                    in_=grouped[:].rearrange("p g r u -> p (g r u)").bitcast(BF16),
+                    out=wa_codes[:, g, P * j : P * j + P].bitcast(FP8X4),
+                    scales=wa_scales[:, g, P * j : P * j + P],
+                    in_=grouped[:, g].rearrange("p r u -> p (r u)").bitcast(BF16),
                 )
-
-            kv_all = front.tile([P, TOKEN_TILES, KV_RANK], F32)
-            pe_all = front.tile([P, TOKEN_TILES, ROPE], F32)
-            gained = front.tile([P, TOKEN_TILES, KV_RANK], F32)
-            junk_kv = front.tile([P, 2, KV_RANK], BF16)
-            junk_gained = front.tile([P, 2, KV_RANK], BF16)
-            sum_kv2 = front.tile([P, TOKEN_TILES], F32)
-            sum_gained2 = front.tile([P, TOKEN_TILES], F32)
-            pe_ps = pe_psum.tile([P, TOKEN_TILES, ROPE], F32)
-            for i in range(TOKEN_TILES):
-                kv_ps = acc_psum.tile([P, BANK], F32, tag="acc")
-                for out_ps, cols in ((kv_ps[:], slice(0, KV_RANK)), (pe_ps[:, i, :], slice(KV_RANK, A_OUT))):
-                    for g in range(PASSES_A):
-                        nc.tensor.matmul_mx(
-                            out=out_ps,
-                            lhsT=x_codes[:, i, P * g : P * g + P].bitcast(FP8X4),
-                            lhsT_scale=x_scales[:, i, P * g : P * g + P],
-                            rhs=wa_codes[:, g, cols].bitcast(FP8X4),
-                            rhs_scale=wa_scales[:, g, cols],
-                            start=(g == 0),
-                            stop=(g == PASSES_A - 1),
-                        )
-                nc.vector.tensor_tensor(out=kv_all[:, i, :], in0=kv_ps[:], in1=bias_a[:, 0:KV_RANK], op=ALU.add)
-                nc.scalar.activation(
-                    out=junk_kv[:, i % 2, :], in_=kv_all[:, i, :], func=ACT.Square, accum_out=sum_kv2[:, i : i + 1]
-                )
-                nc.vector.tensor_tensor(out=gained[:, i, :], in0=kv_all[:, i, :], in1=gain[:], op=ALU.mult)
-                nc.scalar.activation(
-                    out=junk_gained[:, i % 2, :],
-                    in_=gained[:, i, :],
-                    func=ACT.Square,
-                    accum_out=sum_gained2[:, i : i + 1],
-                )
-            nc.vector.tensor_tensor(
-                out=pe_all[:],
-                in0=pe_ps[:],
-                in1=bias_a[:, KV_RANK:A_OUT].unsqueeze(1).to_broadcast([P, TOKEN_TILES, ROPE]),
-                op=ALU.add,
-            )
-
-            rms = front.tile([P, TOKEN_TILES], F32)
-            nc.scalar.activation(out=rms[:], in_=sum_kv2[:], func=ACT.Sqrt, bias=eps_col[:], scale=1.0 / KV_RANK)
-            inv_rms = front.tile([P, TOKEN_TILES], F32)
-            nc.vector.reciprocal(out=inv_rms[:], in_=rms[:])
-            sp_bf = front.tile([P, TOKEN_TILES, KV_RANK], BF16)
-            for i in range(TOKEN_TILES):
-                nc.vector.tensor_scalar(
-                    out=sp_bf[:, i, :], in0=gained[:, i, :], scalar1=inv_rms[:, i : i + 1], scalar2=None, op0=ALU.mult
-                )
-            sum_sp2 = front.tile([P, TOKEN_TILES], F32)
-            nc.vector.tensor_tensor(out=sum_sp2[:], in0=sum_gained2[:], in1=inv_rms[:], op=ALU.mult)
-            nc.vector.tensor_tensor(out=sum_sp2[:], in0=sum_sp2[:], in1=inv_rms[:], op=ALU.mult)
-            nc.scalar.activation(out=time_t[:], in_=sum_sp2[:], func=ACT.Sqrt, bias=one_col[:], scale=1.0)
-
-            sp_grouped = front.tile([P, TOKEN_TILES, P, 4], BF16, align_bytes=64)
-            for pair in range(TOKEN_TILES // 2):
-                sp_turned = turn_psum.tile([P, 2, 4, P], BF16, tag="turned")
-                for i2 in range(2):
-                    for t in range(4):
-                        nc.tensor.transpose(
-                            sp_turned[:, i2, t, :], sp_bf[:, 2 * pair + i2, P * t : P * t + P], ident_bf[:]
-                        )
-                nc.vector.tensor_copy(
-                    out=sp_grouped[:, 2 * pair : 2 * pair + 2], in_=sp_turned[:].rearrange("p i t r -> p i r t")
-                )
+        x_words = x_sb[:].bitcast(F32)
+        for i in range(TOKEN_TILES):
+            grouped = regroup([x_words[:, i, WORDS * g : WORDS * (g + 1)] for g in range(PASSES_A)])
             nc.vector.quantize_mx(
-                out=sp_codes[:].rearrange("p i r -> p (i r)").bitcast(FP8X4),
-                scales=sp_scales[:].rearrange("p i r -> p (i r)"),
-                in_=sp_grouped[:].rearrange("p i r t -> p (i r t)"),
+                out=x_codes[:, i, :].bitcast(FP8X4),
+                scales=x_scales[:, i, :],
+                in_=grouped[:].rearrange("p g r u -> p (g r u)").bitcast(BF16),
             )
 
-            pe_pairs = pe_all[:].rearrange("p i (j two) -> p (i j) two", two=2)
-            even = pe_pairs[:, :, 0].rearrange("p (b hj) -> p b hj", b=2)
-            odd = pe_pairs[:, :, 1].rearrange("p (b hj) -> p b hj", b=2)
-            cos = cos_sb[:].rearrange("p h j -> p (h j)").unsqueeze(1).to_broadcast([P, 2, ROPE])
-            sin = sin_sb[:].rearrange("p h j -> p (h j)").unsqueeze(1).to_broadcast([P, 2, ROPE])
-            even_cos = front.tile([P, 2, ROPE], F32)
-            nc.gpsimd.tensor_tensor(out=even_cos[:], in0=even, in1=cos, op=ALU.mult)
-            odd_sin = front.tile([P, 2, ROPE], F32)
-            nc.gpsimd.tensor_tensor(out=odd_sin[:], in0=odd, in1=sin, op=ALU.mult)
-            even_sin = front.tile([P, 2, ROPE], F32)
-            nc.gpsimd.tensor_tensor(out=even_sin[:], in0=even, in1=sin, op=ALU.mult)
-            odd_cos = front.tile([P, 2, ROPE], F32)
-            nc.gpsimd.tensor_tensor(out=odd_cos[:], in0=odd, in1=cos, op=ALU.mult)
-            k_pe_pairs = k_pe[:].rearrange("p i (j two) -> p (i j) two", two=2)
-            nc.gpsimd.tensor_tensor(
-                out=k_pe_pairs[:, :, 0],
-                in0=even_cos[:].rearrange("p b hj -> p (b hj)"),
-                in1=odd_sin[:].rearrange("p b hj -> p (b hj)"),
-                op=ALU.subtract,
-            )
-            nc.gpsimd.tensor_tensor(
-                out=k_pe_pairs[:, :, 1],
-                in0=even_sin[:].rearrange("p b hj -> p (b hj)"),
-                in1=odd_cos[:].rearrange("p b hj -> p (b hj)"),
-                op=ALU.add,
-            )
-
-            wb_words = wb_sb[:].bitcast(F32)
-            for c in range(B_CHUNKS):
-                cols = slice(BANK * c, BANK * (c + 1))
-                grouped = regroup([wb_words[:, 4 * c + m, 1 : 1 + WORDS] for m in range(4)])
-                nc.vector.quantize_mx(
-                    out=wb_codes[:, cols].bitcast(FP8X4),
-                    scales=wb_scales[:, cols],
-                    in_=grouped[:].rearrange("p m r u -> p (m r u)").bitcast(BF16),
-                )
-                w0_ps = turn_psum.tile([P, BANK], BF16, tag="turned")
-                for m in range(4):
-                    nc.tensor.matmul(
-                        out=w0_ps[:, P * m : P * m + P],
-                        lhsT=wb_sb[:, 4 * c + m, 1:2].to_broadcast([P, P]),
-                        rhs=ident_bf[:],
-                        start=True,
-                        stop=True,
+        kv_all = front.tile([P, TOKEN_TILES, KV_RANK], F32)
+        pe_all = front.tile([P, TOKEN_TILES, ROPE], F32)
+        gained = front.tile([P, TOKEN_TILES, KV_RANK], F32)
+        junk_kv = front.tile([P, 2, KV_RANK], BF16)
+        junk_gained = front.tile([P, 2, KV_RANK], BF16)
+        sum_kv2 = front.tile([P, TOKEN_TILES], F32)
+        sum_gained2 = front.tile([P, TOKEN_TILES], F32)
+        pe_ps = pe_psum.tile([P, TOKEN_TILES, ROPE], F32)
+        for i in range(TOKEN_TILES):
+            kv_ps = acc_psum.tile([P, BANK], F32, tag="acc")
+            for out_ps, cols in ((kv_ps[:], slice(0, KV_RANK)), (pe_ps[:, i, :], slice(KV_RANK, A_OUT))):
+                for g in range(PASSES_A):
+                    nc.tensor.matmul_mx(
+                        out=out_ps,
+                        lhsT=x_codes[:, i, P * g : P * g + P].bitcast(FP8X4),
+                        lhsT_scale=x_scales[:, i, P * g : P * g + P],
+                        rhs=wa_codes[:, g, cols].bitcast(FP8X4),
+                        rhs_scale=wa_scales[:, g, cols],
+                        start=(g == 0),
+                        stop=(g == PASSES_A - 1),
                     )
-                nc.vector.tensor_copy(out=w0_all[:, cols], in_=w0_ps[:])
+            nc.vector.tensor_tensor(out=kv_all[:, i, :], in0=kv_ps[:], in1=bias_a[:, 0:KV_RANK], op=ALU.add)
+            nc.scalar.activation(
+                out=junk_kv[:, i % 2, :], in_=kv_all[:, i, :], func=ACT.Square, accum_out=sum_kv2[:, i : i + 1]
+            )
+            nc.vector.tensor_tensor(out=gained[:, i, :], in0=kv_all[:, i, :], in1=gain[:], op=ALU.mult)
+            nc.scalar.activation(
+                out=junk_gained[:, i % 2, :],
+                in_=gained[:, i, :],
+                func=ACT.Square,
+                accum_out=sum_gained2[:, i : i + 1],
+            )
+        nc.vector.tensor_tensor(
+            out=pe_all[:],
+            in0=pe_ps[:],
+            in1=bias_a[:, KV_RANK:A_OUT].unsqueeze(1).to_broadcast([P, TOKEN_TILES, ROPE]),
+            op=ALU.add,
+        )
 
-        with tc.tile_pool(name="back", bufs=2) as back:
-            k_rows = out_0.rearrange("b s h c -> (b s) (h c)")
-            v_rows = out_1.rearrange("b s h c -> (b s) (h c)")
-            junk_head = back.tile([P, 4, V_DIM], BF16, bufs=1)
-            for i in range(TOKEN_TILES):
-                k_out = back.tile([P, HEADS, 1 + NOPE + ROPE], F32)
-                v_out = back.tile([P, HEADS, 1 + V_DIM], F32)
-                nc.gpsimd.tensor_scalar(
-                    out=k_out[:, :, 1 + NOPE :],
-                    in0=k_pe[:, i, :].unsqueeze(1).to_broadcast([P, HEADS, ROPE]),
-                    scalar1=1.0,
-                    scalar2=0.0,
-                    op0=ALU.mult,
-                    op1=ALU.add,
+        rms = front.tile([P, TOKEN_TILES], F32)
+        nc.scalar.activation(out=rms[:], in_=sum_kv2[:], func=ACT.Sqrt, bias=eps_col[:], scale=1.0 / KV_RANK)
+        inv_rms = front.tile([P, TOKEN_TILES], F32)
+        nc.vector.reciprocal(out=inv_rms[:], in_=rms[:])
+        sp_bf = front.tile([P, TOKEN_TILES, KV_RANK], BF16)
+        for i in range(TOKEN_TILES):
+            nc.vector.tensor_scalar(
+                out=sp_bf[:, i, :], in0=gained[:, i, :], scalar1=inv_rms[:, i : i + 1], scalar2=None, op0=ALU.mult
+            )
+        sum_sp2 = front.tile([P, TOKEN_TILES], F32)
+        nc.vector.tensor_tensor(out=sum_sp2[:], in0=sum_gained2[:], in1=inv_rms[:], op=ALU.mult)
+        nc.vector.tensor_tensor(out=sum_sp2[:], in0=sum_sp2[:], in1=inv_rms[:], op=ALU.mult)
+        nc.scalar.activation(out=time_t[:], in_=sum_sp2[:], func=ACT.Sqrt, bias=one_col[:], scale=1.0)
+
+        sp_grouped = front.tile([P, TOKEN_TILES, P, 4], BF16, align_bytes=64)
+        for pair in range(TOKEN_TILES // 2):
+            sp_turned = turn_psum.tile([P, 2, 4, P], BF16, tag="turned")
+            for i2 in range(2):
+                for t in range(4):
+                    nc.tensor.transpose(
+                        sp_turned[:, i2, t, :], sp_bf[:, 2 * pair + i2, P * t : P * t + P], ident_bf[:]
+                    )
+            nc.vector.tensor_copy(
+                out=sp_grouped[:, 2 * pair : 2 * pair + 2], in_=sp_turned[:].rearrange("p i t r -> p i r t")
+            )
+        nc.vector.quantize_mx(
+            out=sp_codes[:].rearrange("p i r -> p (i r)").bitcast(FP8X4),
+            scales=sp_scales[:].rearrange("p i r -> p (i r)"),
+            in_=sp_grouped[:].rearrange("p i r t -> p (i r t)"),
+        )
+
+        pe_pairs = pe_all[:].rearrange("p i (j two) -> p (i j) two", two=2)
+        even = pe_pairs[:, :, 0].rearrange("p (b hj) -> p b hj", b=2)
+        odd = pe_pairs[:, :, 1].rearrange("p (b hj) -> p b hj", b=2)
+        cos = cos_sb[:].rearrange("p h j -> p (h j)").unsqueeze(1).to_broadcast([P, 2, ROPE])
+        sin = sin_sb[:].rearrange("p h j -> p (h j)").unsqueeze(1).to_broadcast([P, 2, ROPE])
+        even_cos = front.tile([P, 2, ROPE], F32)
+        nc.gpsimd.tensor_tensor(out=even_cos[:], in0=even, in1=cos, op=ALU.mult)
+        odd_sin = front.tile([P, 2, ROPE], F32)
+        nc.gpsimd.tensor_tensor(out=odd_sin[:], in0=odd, in1=sin, op=ALU.mult)
+        even_sin = front.tile([P, 2, ROPE], F32)
+        nc.gpsimd.tensor_tensor(out=even_sin[:], in0=even, in1=sin, op=ALU.mult)
+        odd_cos = front.tile([P, 2, ROPE], F32)
+        nc.gpsimd.tensor_tensor(out=odd_cos[:], in0=odd, in1=cos, op=ALU.mult)
+        k_pe_pairs = k_pe[:].rearrange("p i (j two) -> p (i j) two", two=2)
+        nc.gpsimd.tensor_tensor(
+            out=k_pe_pairs[:, :, 0],
+            in0=even_cos[:].rearrange("p b hj -> p (b hj)"),
+            in1=odd_sin[:].rearrange("p b hj -> p (b hj)"),
+            op=ALU.subtract,
+        )
+        nc.gpsimd.tensor_tensor(
+            out=k_pe_pairs[:, :, 1],
+            in0=even_sin[:].rearrange("p b hj -> p (b hj)"),
+            in1=odd_cos[:].rearrange("p b hj -> p (b hj)"),
+            op=ALU.add,
+        )
+
+        wb_words = wb_sb[:].bitcast(F32)
+        for c in range(B_CHUNKS):
+            cols = slice(BANK * c, BANK * (c + 1))
+            grouped = regroup([wb_words[:, 4 * c + m, 1 : 1 + WORDS] for m in range(4)])
+            nc.vector.quantize_mx(
+                out=wb_codes[:, cols].bitcast(FP8X4),
+                scales=wb_scales[:, cols],
+                in_=grouped[:].rearrange("p m r u -> p (m r u)").bitcast(BF16),
+            )
+            w0_ps = turn_psum.tile([P, BANK], BF16, tag="turned")
+            for m in range(4):
+                nc.tensor.matmul(
+                    out=w0_ps[:, P * m : P * m + P],
+                    lhsT=wb_sb[:, 4 * c + m, 1:2].to_broadcast([P, P]),
+                    rhs=ident_bf[:],
+                    start=True,
+                    stop=True,
                 )
-                sum_pe2 = back.tile([P, 1], F32)
-                nc.scalar.activation(
-                    out=junk_head[:, 0, :], in_=k_out[:, 0, 1 + NOPE :], func=ACT.Square, accum_out=sum_pe2[:]
-                )
-                pe_norm = back.tile([P, 1], F32)
-                nc.gpsimd.tensor_scalar(
-                    out=pe_norm[:], in0=sum_pe2[:], scalar1=1.0, scalar2=1.0, op0=ALU.mult, op1=ALU.add
-                )
-                y = back.tile([P, HEADS, HEAD_ROWS], F32)
+            nc.scalar.copy(out=w0_all[:, cols], in_=w0_ps[:])
+
+        k_rows = out_0.rearrange("b s h c -> (b s) h c")
+        v_rows = out_1.rearrange("b s h c -> (b s) h c")
+        junk_head = keep.tile([P, 4, V_DIM], BF16)
+        HALF_HEADS = HEADS // 2
+        HALF_BANKS = B_CHUNKS // 2
+
+        def second_stage(i):
+            k_out = back.tile([P, HEADS, 1 + NOPE + ROPE], F32)
+            v_out = back.tile([P, HEADS, 1 + V_DIM], F32)
+            nc.gpsimd.tensor_scalar(
+                out=k_out[:, :, 1 + NOPE :],
+                in0=k_pe[:, i, :].unsqueeze(1).to_broadcast([P, HEADS, ROPE]),
+                scalar1=1.0,
+                scalar2=0.0,
+                op0=ALU.mult,
+                op1=ALU.add,
+            )
+            sum_pe2 = back.tile([P, 1], F32)
+            nc.scalar.activation(
+                out=junk_head[:, 0, :], in_=k_out[:, 0, 1 + NOPE :], func=ACT.Square, accum_out=sum_pe2[:]
+            )
+            pe_norm = back.tile([P, 1], F32)
+            nc.gpsimd.tensor_scalar(out=pe_norm[:], in0=sum_pe2[:], scalar1=1.0, scalar2=1.0, op0=ALU.mult, op1=ALU.add)
+            sum_k2 = back.tile([P, HEADS], F32)
+            sum_v2 = back.tile([P, HEADS], F32)
+            for half in range(2):
+                heads = slice(HALF_HEADS * half, HALF_HEADS * (half + 1))
+                y = back.tile([P, HALF_HEADS, HEAD_ROWS], F32)
                 y_flat = y[:].rearrange("p h f -> p (h f)")
-                for c in range(B_CHUNKS):
+                for n in range(HALF_BANKS):
+                    c = HALF_BANKS * half + n
                     cols = slice(BANK * c, BANK * (c + 1))
                     y_ps = acc_psum.tile([P, BANK], F32, tag="acc")
                     nc.tensor.matmul_mx(
@@ -316,37 +322,36 @@ def tile_lorentzmla_pa_kernel(
                         stop=True,
                     )
                     nc.vector.scalar_tensor_tensor(
-                        out=y_flat[:, cols],
+                        out=y_flat[:, BANK * n : BANK * (n + 1)],
                         in0=w0_all[:, cols],
                         scalar=time_t[:, i : i + 1],
                         in1=y_ps[:],
                         op0=ALU.mult,
                         op1=ALU.add,
                     )
-                sum_k2 = back.tile([P, HEADS], F32)
-                sum_v2 = back.tile([P, HEADS], F32)
-                for heads in (slice(0, HEADS // 2), slice(HEADS // 2, HEADS)):
-                    nc.gpsimd.tensor_tensor(
-                        out=k_out[:, heads, 1 : 1 + NOPE], in0=y[:, heads, 0:NOPE], in1=bias_b[:, heads, 0:NOPE], op=ALU.add
-                    )
-                    nc.vector.tensor_tensor(
-                        out=v_out[:, heads, 1:], in0=y[:, heads, NOPE:], in1=bias_b[:, heads, NOPE:], op=ALU.add
-                    )
-                for h in range(HEADS):
+                nc.gpsimd.tensor_tensor(
+                    out=k_out[:, heads, 1 : 1 + NOPE], in0=y[:, :, 0:NOPE], in1=bias_b[:, heads, 0:NOPE], op=ALU.add
+                )
+                nc.vector.tensor_tensor(out=v_out[:, heads, 1:], in0=y[:, :, NOPE:], in1=bias_b[:, heads, NOPE:], op=ALU.add)
+                for h in range(HALF_HEADS * half, HALF_HEADS * (half + 1)):
                     nc.scalar.activation(
-                        out=junk_head[:, h % 4, :],
-                        in_=v_out[:, h, 1:],
-                        func=ACT.Square,
-                        accum_out=sum_v2[:, h : h + 1],
+                        out=junk_head[:, h % 4, :], in_=v_out[:, h, 1:], func=ACT.Square, accum_out=sum_v2[:, h : h + 1]
                     )
-                nc.scalar.activation(out=v_out[:, :, 0], in_=sum_v2[:], func=ACT.Sqrt, bias=one_col[:], scale=1.0)
-                nc.sync.dma_start(out=v_rows[P * i : P * i + P, :], in_=v_out[:].rearrange("p h c -> p (h c)"))
-                for h in range(HEADS):
+                nc.scalar.activation(
+                    out=v_out[:, heads, 0], in_=sum_v2[:, heads], func=ACT.Sqrt, bias=one_col[:], scale=1.0
+                )
+                nc.sync.dma_start(out=v_rows[P * i : P * i + P, heads, :], in_=v_out[:, heads, :])
+                for h in range(HALF_HEADS * half, HALF_HEADS * (half + 1)):
                     nc.scalar.activation(
                         out=junk_head[:, h % 4, 0:NOPE],
                         in_=k_out[:, h, 1 : 1 + NOPE],
                         func=ACT.Square,
                         accum_out=sum_k2[:, h : h + 1],
                     )
-                nc.scalar.activation(out=k_out[:, :, 0], in_=sum_k2[:], func=ACT.Sqrt, bias=pe_norm[:], scale=1.0)
-                nc.sync.dma_start(out=k_rows[P * i : P * i + P, :], in_=k_out[:].rearrange("p h c -> p (h c)"))
+                nc.scalar.activation(
+                    out=k_out[:, heads, 0], in_=sum_k2[:, heads], func=ACT.Sqrt, bias=pe_norm[:], scale=1.0
+                )
+                nc.sync.dma_start(out=k_rows[P * i : P * i + P, heads, :], in_=k_out[:, heads, :])
+
+        for i in range(TOKEN_TILES):
+            second_stage(i)

@@ -58,7 +58,7 @@ def tile_lorentzmla_pa_kernel(
         sp_scales = keep.tile([P, TOKEN_TILES, P], U8, align_bytes=64)
         wb_codes = keep.tile([P, B_OUT], U32, align_bytes=64)
         wb_scales = keep.tile([P, B_OUT], U8, align_bytes=64)
-        w0_all = keep.tile([P, B_OUT], BF16)
+        w0_all = keep.tile([P, 2 + B_OUT], BF16)
         bias_b = keep.tile([P, HEADS, HEAD_ROWS], BF16)
         time_t = keep.tile([P, TOKEN_TILES], F32)
         k_pe = keep.tile([P, TOKEN_TILES, ROPE], F32)
@@ -107,11 +107,25 @@ def tile_lorentzmla_pa_kernel(
         for i in range(TOKEN_TILES):
             nc.sync.dma_start(out=x_sb[:, i, :], in_=x_rows[P * i : P * i + P, :])
         wb_sb = front.tile([P, B_TILES, ROW_SLOT], BF16)
-        wb_rows = wkv_b_w.rearrange("(n p) c -> p n c", p=P)
+        wb_flat = wkv_b_w.rearrange("r c -> (r c)")
+        RUN = KV_RANK + 1
+        FULL_TILES = B_TILES - 1
+        wb_runs = wb_flat[1 : 1 + FULL_TILES * P * RUN].rearrange("(n p c) -> p n c", p=P, c=RUN)
         for c in range(B_CHUNKS):
-            nc.sync.dma_start(
-                out=wb_sb[:, 4 * c : 4 * c + 4, 1 : 1 + KV_RANK + 1], in_=wb_rows[:, 4 * c : 4 * c + 4, :]
-            )
+            last = min(4 * c + 4, FULL_TILES)
+            nc.sync.dma_start(out=wb_sb[:, 4 * c : last, 0:RUN], in_=wb_runs[:, 4 * c : last, :])
+        tail0 = 1 + FULL_TILES * P * RUN
+        nc.sync.dma_start(
+            out=wb_sb[0 : P - 1, FULL_TILES, 0:RUN],
+            in_=wb_flat[tail0 : tail0 + (P - 1) * RUN].rearrange("(p c) -> p c", c=RUN),
+        )
+        nc.sync.dma_start(
+            out=wb_sb[P - 1 : P, FULL_TILES, 0:KV_RANK],
+            in_=wb_flat[tail0 + (P - 1) * RUN : tail0 + (P - 1) * RUN + KV_RANK].rearrange("(p c) -> p c", p=1),
+        )
+        nc.sync.dma_start(
+            out=wb_sb[P - 1 : P, FULL_TILES, KV_RANK:RUN], in_=wb_flat[0:1].rearrange("(p c) -> p c", p=1)
+        )
         cos_sb = front.tile([P, 2, ROPE // 2], BF16)
         nc.sync.dma_start(out=cos_sb[:], in_=freqs_cos.rearrange("(h p) j -> p h j", p=P))
         sin_sb = front.tile([P, 2, ROPE // 2], BF16)
@@ -262,7 +276,7 @@ def tile_lorentzmla_pa_kernel(
         wb_words = wb_sb[:].bitcast(F32)
         for c in range(B_CHUNKS):
             cols = slice(BANK * c, BANK * (c + 1))
-            grouped = regroup([wb_words[:, 4 * c + m, 1 : 1 + WORDS] for m in range(4)])
+            grouped = regroup([wb_words[:, 4 * c + m, 0:WORDS] for m in range(4)])
             nc.vector.quantize_mx(
                 out=wb_codes[:, cols].bitcast(FP8X4),
                 scales=wb_scales[:, cols],
@@ -272,12 +286,16 @@ def tile_lorentzmla_pa_kernel(
             for m in range(4):
                 nc.tensor.matmul(
                     out=w0_ps[:, P * m : P * m + P],
-                    lhsT=wb_sb[:, 4 * c + m, 1:2].to_broadcast([P, P]),
+                    lhsT=wb_sb[:, 4 * c + m, KV_RANK:RUN].to_broadcast([P, P]),
                     rhs=ident_bf[:],
                     start=True,
                     stop=True,
                 )
-            nc.scalar.copy(out=w0_all[:, cols], in_=w0_ps[:])
+            if c < B_CHUNKS - 1:
+                nc.scalar.copy(out=w0_all[:, 2 + BANK * c : 2 + BANK * (c + 1)], in_=w0_ps[:])
+            else:
+                nc.scalar.copy(out=w0_all[:, 2 + BANK * c : 1 + B_OUT], in_=w0_ps[:, 0 : BANK - 1])
+                nc.scalar.copy(out=w0_all[:, 1:2], in_=w0_ps[:, BANK - 1 : BANK])
 
         k_rows = out_0.rearrange("b s h c -> (b s) h c")
         v_rows = out_1.rearrange("b s h c -> (b s) h c")
@@ -323,7 +341,7 @@ def tile_lorentzmla_pa_kernel(
                     )
                     nc.vector.scalar_tensor_tensor(
                         out=y_flat[:, BANK * n : BANK * (n + 1)],
-                        in0=w0_all[:, cols],
+                        in0=w0_all[:, 1 + BANK * c : 1 + BANK * (c + 1)],
                         scalar=time_t[:, i : i + 1],
                         in1=y_ps[:],
                         op0=ALU.mult,

@@ -297,10 +297,23 @@ def tile_lorentzmla_pa_kernel(
                 nc.scalar.copy(out=w0_all[:, 2 + BANK * c : 1 + B_OUT], in_=w0_ps[:, 0 : BANK - 1])
                 nc.scalar.copy(out=w0_all[:, 1:2], in_=w0_ps[:, BANK - 1 : BANK])
 
+        HALF_HEADS = HEADS // 2
+        bias_v_halves = []
+        for half in range(2):
+            bias_v_ps = turn_psum.tile([P, HALF_HEADS, V_DIM], BF16, tag="turned")
+            for q in range(HALF_HEADS):
+                nc.tensor.matmul(
+                    out=bias_v_ps[:, q, :],
+                    lhsT=ident_bf[:, 0:1].to_broadcast([P, P]),
+                    rhs=bias_b[:, HALF_HEADS * half + q, NOPE:],
+                    start=True,
+                    stop=True,
+                )
+            bias_v_halves.append(bias_v_ps)
+
         k_rows = out_0.rearrange("b s h c -> (b s) h c")
         v_rows = out_1.rearrange("b s h c -> (b s) h c")
         junk_head = keep.tile([P, 4, V_DIM], BF16)
-        HALF_HEADS = HEADS // 2
         HALF_BANKS = B_CHUNKS // 2
 
         def second_stage(i):
@@ -350,7 +363,7 @@ def tile_lorentzmla_pa_kernel(
                 nc.gpsimd.tensor_tensor(
                     out=k_out[:, heads, 1 : 1 + NOPE], in0=y[:, :, 0:NOPE], in1=bias_b[:, heads, 0:NOPE], op=ALU.add
                 )
-                nc.vector.tensor_tensor(out=v_out[:, heads, 1:], in0=y[:, :, NOPE:], in1=bias_b[:, heads, NOPE:], op=ALU.add)
+                nc.vector.tensor_tensor(out=v_out[:, heads, 1:], in0=y[:, :, NOPE:], in1=bias_v_halves[half][:], op=ALU.add)
                 for h in range(HALF_HEADS * half, HALF_HEADS * (half + 1)):
                     nc.scalar.activation(
                         out=junk_head[:, h % 4, :], in_=v_out[:, h, 1:], func=ACT.Square, accum_out=sum_v2[:, h : h + 1]

@@ -59,7 +59,7 @@ def tile_lorentzmla_pa_kernel(
         wb_codes = keep.tile([P, B_OUT], U32, align_bytes=64)
         wb_scales = keep.tile([P, B_OUT], U8, align_bytes=64)
         w0_all = keep.tile([P, 2 + B_OUT], BF16)
-        bias_b = keep.tile([P, HEADS, HEAD_ROWS], BF16)
+        bias_k = keep.tile([P, HEADS, NOPE], BF16)
         time_t = keep.tile([P, TOKEN_TILES], F32)
         k_pe = keep.tile([P, TOKEN_TILES, ROPE], F32)
 
@@ -88,14 +88,22 @@ def tile_lorentzmla_pa_kernel(
                 )
             return grouped
 
-        A_ROW0, G_ROW0 = 0, 32
-        vec_rows = front.tile([P, P], BF16)
+        A_ROW0, G_ROW0, BV_ROW0, BK_ROW0 = 0, 32, 64, 96
+        vec_rows = keep.tile([P, P], BF16)
         nc.vector.memset(vec_rows[:], 0.0)
         nc.sync.dma_start(
             out=vec_rows[A_ROW0 : A_ROW0 + A_TILES, :], in_=wkv_a_b.rearrange("(r c) -> r c", c=P)
         )
         nc.sync.dma_start(
             out=vec_rows[G_ROW0 : G_ROW0 + KV_RANK // P, :], in_=kv_norm_w.rearrange("(r c) -> r c", c=P)
+        )
+        nc.sync.dma_start(
+            out=vec_rows[BV_ROW0 : BV_ROW0 + HEADS, :],
+            in_=wkv_b_b.rearrange("(h f) -> h f", f=HEAD_ROWS)[:, NOPE:HEAD_ROWS],
+        )
+        nc.sync.dma_start(
+            out=vec_rows[BK_ROW0 : BK_ROW0 + HEADS // 2, :].rearrange("r (two f) -> r two f", two=2),
+            in_=wkv_b_b.rearrange("(r two f) -> r two f", two=2, f=HEAD_ROWS)[:, :, 0:NOPE],
         )
         wa_sb = front.tile([P, A_TILES, DIM], BF16)
         kv_rows = wkv_a_w[0:KV_RANK, :].rearrange("(u q e) k -> u e q k", u=2, e=2)
@@ -106,6 +114,10 @@ def tile_lorentzmla_pa_kernel(
         x_rows = x.rearrange("b s k -> (b s) k")
         for i in range(TOKEN_TILES):
             nc.sync.dma_start(out=x_sb[:, i, :], in_=x_rows[P * i : P * i + P, :])
+        cos_sb = front.tile([P, 2, ROPE // 2], BF16)
+        nc.sync.dma_start(out=cos_sb[:], in_=freqs_cos.rearrange("(h p) j -> p h j", p=P))
+        sin_sb = front.tile([P, 2, ROPE // 2], BF16)
+        nc.sync.dma_start(out=sin_sb[:], in_=freqs_sin.rearrange("(h p) j -> p h j", p=P))
         wb_sb = front.tile([P, B_TILES, ROW_SLOT], BF16)
         wb_flat = wkv_b_w.rearrange("r c -> (r c)")
         RUN = KV_RANK + 1
@@ -126,11 +138,6 @@ def tile_lorentzmla_pa_kernel(
         nc.sync.dma_start(
             out=wb_sb[P - 1 : P, FULL_TILES, KV_RANK:RUN], in_=wb_flat[0:1].rearrange("(p c) -> p c", p=1)
         )
-        cos_sb = front.tile([P, 2, ROPE // 2], BF16)
-        nc.sync.dma_start(out=cos_sb[:], in_=freqs_cos.rearrange("(h p) j -> p h j", p=P))
-        sin_sb = front.tile([P, 2, ROPE // 2], BF16)
-        nc.sync.dma_start(out=sin_sb[:], in_=freqs_sin.rearrange("(h p) j -> p h j", p=P))
-        nc.sync.dma_start(out=bias_b[:].rearrange("p h f -> p (h f)"), in_=wkv_b_b.partition_broadcast(P))
 
         def spread_rows(first_row, n_rows):
             spread = turn_psum.tile([P, 2 * BANK], BF16, tag="turned")
@@ -157,6 +164,9 @@ def tile_lorentzmla_pa_kernel(
             out=gain[:].rearrange("p (u e q) -> p u e q", u=2, e=2),
             in_=spread_g[:, 0:KV_RANK].rearrange("p (u q e) -> p u e q", u=2, e=2),
         )
+
+        spread_k = spread_rows(BK_ROW0, HEADS // 2)
+        nc.vector.tensor_copy(out=bias_k[:].rearrange("p h f -> p (h f)"), in_=spread_k[:])
 
         wa_words = wa_sb[:].bitcast(F32)
         for j in range(A_TILES):
@@ -298,18 +308,7 @@ def tile_lorentzmla_pa_kernel(
                 nc.scalar.copy(out=w0_all[:, 1:2], in_=w0_ps[:, BANK - 1 : BANK])
 
         HALF_HEADS = HEADS // 2
-        bias_v_halves = []
-        for half in range(2):
-            bias_v_ps = turn_psum.tile([P, HALF_HEADS, V_DIM], BF16, tag="turned")
-            for q in range(HALF_HEADS):
-                nc.tensor.matmul(
-                    out=bias_v_ps[:, q, :],
-                    lhsT=ident_bf[:, 0:1].to_broadcast([P, P]),
-                    rhs=bias_b[:, HALF_HEADS * half + q, NOPE:],
-                    start=True,
-                    stop=True,
-                )
-            bias_v_halves.append(bias_v_ps)
+        bias_v_halves = [spread_rows(BV_ROW0 + HALF_HEADS * half, HALF_HEADS) for half in range(2)]
 
         k_rows = out_0.rearrange("b s h c -> (b s) h c")
         v_rows = out_1.rearrange("b s h c -> (b s) h c")
@@ -361,9 +360,9 @@ def tile_lorentzmla_pa_kernel(
                         op1=ALU.add,
                     )
                 nc.gpsimd.tensor_tensor(
-                    out=k_out[:, heads, 1 : 1 + NOPE], in0=y[:, :, 0:NOPE], in1=bias_b[:, heads, 0:NOPE], op=ALU.add
+                    out=k_out[:, heads, 1 : 1 + NOPE], in0=y[:, :, 0:NOPE], in1=bias_k[:, heads, :], op=ALU.add
                 )
-                nc.vector.tensor_tensor(out=v_out[:, heads, 1:], in0=y[:, :, NOPE:], in1=bias_v_halves[half][:], op=ALU.add)
+                nc.vector.tensor_tensor(out=v_out[:, heads, 1:], in0=y[:, :, NOPE:], in1=bias_v_halves[half][:].rearrange("p (h f) -> p h f", f=V_DIM), op=ALU.add)
                 for h in range(HALF_HEADS * half, HALF_HEADS * (half + 1)):
                     nc.scalar.activation(
                         out=junk_head[:, h % 4, :], in_=v_out[:, h, 1:], func=ACT.Square, accum_out=sum_v2[:, h : h + 1]

@@ -46,6 +46,7 @@ def tile_lorentzmla_pa_kernel(
         front = ctx.enter_context(tc.tile_pool(name="front", bufs=1))
         stage = ctx.enter_context(tc.tile_pool(name="stage", bufs=3))
         back = ctx.enter_context(tc.tile_pool(name="back", bufs=2))
+        outs = ctx.enter_context(tc.tile_pool(name="outs", bufs=4))
         turn_psum = ctx.enter_context(tc.psum_pool(name="turn_psum", bufs=4))
         acc_psum = ctx.enter_context(tc.psum_pool(name="acc_psum", bufs=3))
         pe_psum = ctx.enter_context(tc.psum_pool(name="pe_psum", bufs=1))
@@ -123,9 +124,6 @@ def tile_lorentzmla_pa_kernel(
         RUN = KV_RANK + 1
         FULL_TILES = B_TILES - 1
         wb_runs = wb_flat[1 : 1 + FULL_TILES * P * RUN].rearrange("(n p c) -> p n c", p=P, c=RUN)
-        for c in range(B_CHUNKS):
-            last = min(4 * c + 4, FULL_TILES)
-            nc.sync.dma_start(out=wb_sb[:, 4 * c : last, 0:RUN], in_=wb_runs[:, 4 * c : last, :])
         tail0 = 1 + FULL_TILES * P * RUN
         nc.sync.dma_start(
             out=wb_sb[0 : P - 1, FULL_TILES, 0:RUN],
@@ -138,9 +136,12 @@ def tile_lorentzmla_pa_kernel(
         nc.sync.dma_start(
             out=wb_sb[P - 1 : P, FULL_TILES, KV_RANK:RUN], in_=wb_flat[0:1].rearrange("(p c) -> p c", p=1)
         )
+        for c in range(B_CHUNKS):
+            last = min(4 * c + 4, FULL_TILES)
+            nc.sync.dma_start(out=wb_sb[:, 4 * c : last, 0:RUN], in_=wb_runs[:, 4 * c : last, :])
 
-        def spread_rows(first_row, n_rows):
-            spread = turn_psum.tile([P, 2 * BANK], BF16, tag="turned")
+        def spread_rows(first_row, n_rows, pool, tag):
+            spread = pool.tile([P, 2 * BANK], BF16, tag=tag)
             for r in range(n_rows):
                 nc.tensor.matmul(
                     out=spread[:, P * r : P * r + P],
@@ -152,20 +153,20 @@ def tile_lorentzmla_pa_kernel(
             return spread
 
         bias_a = front.tile([P, A_OUT], BF16)
-        spread_a = spread_rows(A_ROW0, A_TILES)
+        spread_a = spread_rows(A_ROW0, A_TILES, turn_psum, "turned")
         nc.vector.tensor_copy(
             out=bias_a[:, 0:KV_RANK].rearrange("p (u e q) -> p u e q", u=2, e=2),
             in_=spread_a[:, 0:KV_RANK].rearrange("p (u q e) -> p u e q", u=2, e=2),
         )
         nc.vector.tensor_copy(out=bias_a[:, KV_RANK:A_OUT], in_=spread_a[:, KV_RANK:A_OUT])
         gain = front.tile([P, KV_RANK], BF16)
-        spread_g = spread_rows(G_ROW0, KV_RANK // P)
+        spread_g = spread_rows(G_ROW0, KV_RANK // P, turn_psum, "turned")
         nc.vector.tensor_copy(
             out=gain[:].rearrange("p (u e q) -> p u e q", u=2, e=2),
             in_=spread_g[:, 0:KV_RANK].rearrange("p (u q e) -> p u e q", u=2, e=2),
         )
 
-        spread_k = spread_rows(BK_ROW0, HEADS // 2)
+        spread_k = spread_rows(BK_ROW0, HEADS // 2, turn_psum, "turned")
         nc.vector.tensor_copy(out=bias_k[:].rearrange("p h f -> p (h f)"), in_=spread_k[:])
 
         wa_words = wa_sb[:].bitcast(F32)
@@ -193,7 +194,7 @@ def tile_lorentzmla_pa_kernel(
         junk_gained = front.tile([P, 2, KV_RANK], BF16)
         sum_kv2 = front.tile([P, TOKEN_TILES], F32)
         sum_gained2 = front.tile([P, TOKEN_TILES], F32)
-        pe_ps = pe_psum.tile([P, TOKEN_TILES, ROPE], F32)
+        pe_ps = pe_psum.tile([P, TOKEN_TILES, ROPE], F32, tag="pe")
         for i in range(TOKEN_TILES):
             kv_ps = acc_psum.tile([P, BANK], F32, tag="acc")
             for out_ps, cols in ((kv_ps[:], slice(0, KV_RANK)), (pe_ps[:, i, :], slice(KV_RANK, A_OUT))):
@@ -284,7 +285,22 @@ def tile_lorentzmla_pa_kernel(
         )
 
         wb_words = wb_sb[:].bitcast(F32)
-        for c in range(B_CHUNKS):
+        HALF_HEADS = HEADS // 2
+        HALF_BANKS = B_CHUNKS // 2
+
+        def spread_w0(row_tiles):
+            w0_ps = turn_psum.tile([P, BANK], BF16, tag="turned")
+            for m, n in enumerate(row_tiles):
+                nc.tensor.matmul(
+                    out=w0_ps[:, P * m : P * m + P],
+                    lhsT=wb_sb[:, n, KV_RANK:RUN].to_broadcast([P, P]),
+                    rhs=ident_bf[:],
+                    start=True,
+                    stop=True,
+                )
+            return w0_ps
+
+        def prepare_wb(c):
             cols = slice(BANK * c, BANK * (c + 1))
             grouped = regroup([wb_words[:, 4 * c + m, 0:WORDS] for m in range(4)])
             nc.vector.quantize_mx(
@@ -292,96 +308,92 @@ def tile_lorentzmla_pa_kernel(
                 scales=wb_scales[:, cols],
                 in_=grouped[:].rearrange("p m r u -> p (m r u)").bitcast(BF16),
             )
-            w0_ps = turn_psum.tile([P, BANK], BF16, tag="turned")
-            for m in range(4):
-                nc.tensor.matmul(
-                    out=w0_ps[:, P * m : P * m + P],
-                    lhsT=wb_sb[:, 4 * c + m, KV_RANK:RUN].to_broadcast([P, P]),
-                    rhs=ident_bf[:],
-                    start=True,
-                    stop=True,
-                )
-            if c < B_CHUNKS - 1:
-                nc.scalar.copy(out=w0_all[:, 2 + BANK * c : 2 + BANK * (c + 1)], in_=w0_ps[:])
-            else:
-                nc.scalar.copy(out=w0_all[:, 2 + BANK * c : 1 + B_OUT], in_=w0_ps[:, 0 : BANK - 1])
-                nc.scalar.copy(out=w0_all[:, 1:2], in_=w0_ps[:, BANK - 1 : BANK])
+            w0_ps = spread_w0(range(4 * c, 4 * c + 4))
+            width = min(BANK, B_OUT - 1 - BANK * c)
+            nc.scalar.copy(out=w0_all[:, 2 + BANK * c : 2 + BANK * c + width], in_=w0_ps[:, 0:width])
 
-        HALF_HEADS = HEADS // 2
-        bias_v_halves = [spread_rows(BV_ROW0 + HALF_HEADS * half, HALF_HEADS) for half in range(2)]
+        wrap_ps = spread_w0([B_TILES - 1])
+        nc.scalar.copy(out=w0_all[:, 1:2], in_=wrap_ps[:, P - 1 : P])
 
         k_rows = out_0.rearrange("b s h c -> (b s) h c")
         v_rows = out_1.rearrange("b s h c -> (b s) h c")
         junk_head = keep.tile([P, 4, V_DIM], BF16)
-        HALF_BANKS = B_CHUNKS // 2
+        sum_pe2 = keep.tile([P, TOKEN_TILES], F32)
+        for i in range(TOKEN_TILES):
+            nc.scalar.activation(
+                out=junk_head[:, i, :], in_=k_pe[:, i, :], func=ACT.Square, accum_out=sum_pe2[:, i : i + 1]
+            )
+        pe_norm = keep.tile([P, TOKEN_TILES], F32)
+        nc.gpsimd.tensor_scalar(out=pe_norm[:], in0=sum_pe2[:], scalar1=1.0, scalar2=1.0, op0=ALU.mult, op1=ALU.add)
 
-        def second_stage(i):
-            k_out = back.tile([P, HEADS, 1 + NOPE + ROPE], F32)
-            v_out = back.tile([P, HEADS, 1 + V_DIM], F32)
+        def second_stage(i, half, bias_v):
+            heads = slice(HALF_HEADS * half, HALF_HEADS * (half + 1))
+            k_out = outs.tile([P, HALF_HEADS, 1 + NOPE + ROPE], F32)
+            v_out = outs.tile([P, HALF_HEADS, 1 + V_DIM], F32)
+            sum_k2 = outs.tile([P, HALF_HEADS], F32)
+            sum_v2 = outs.tile([P, HALF_HEADS], F32)
             nc.gpsimd.tensor_scalar(
                 out=k_out[:, :, 1 + NOPE :],
-                in0=k_pe[:, i, :].unsqueeze(1).to_broadcast([P, HEADS, ROPE]),
+                in0=k_pe[:, i, :].unsqueeze(1).to_broadcast([P, HALF_HEADS, ROPE]),
                 scalar1=1.0,
                 scalar2=0.0,
                 op0=ALU.mult,
                 op1=ALU.add,
             )
-            sum_pe2 = back.tile([P, 1], F32)
-            nc.scalar.activation(
-                out=junk_head[:, 0, :], in_=k_out[:, 0, 1 + NOPE :], func=ACT.Square, accum_out=sum_pe2[:]
+            y = back.tile([P, HALF_HEADS, HEAD_ROWS], F32)
+            y_flat = y[:].rearrange("p h f -> p (h f)")
+            for n in range(HALF_BANKS):
+                c = HALF_BANKS * half + n
+                cols = slice(BANK * c, BANK * (c + 1))
+                y_ps = acc_psum.tile([P, BANK], F32, tag="acc")
+                nc.tensor.matmul_mx(
+                    out=y_ps[:],
+                    lhsT=sp_codes[:, i, :].bitcast(FP8X4),
+                    lhsT_scale=sp_scales[:, i, :],
+                    rhs=wb_codes[:, cols].bitcast(FP8X4),
+                    rhs_scale=wb_scales[:, cols],
+                    start=True,
+                    stop=True,
+                )
+                nc.vector.scalar_tensor_tensor(
+                    out=y_flat[:, BANK * n : BANK * (n + 1)],
+                    in0=w0_all[:, 1 + BANK * c : 1 + BANK * (c + 1)],
+                    scalar=time_t[:, i : i + 1],
+                    in1=y_ps[:],
+                    op0=ALU.mult,
+                    op1=ALU.add,
+                )
+            nc.gpsimd.tensor_tensor(
+                out=k_out[:, :, 1 : 1 + NOPE], in0=y[:, :, 0:NOPE], in1=bias_k[:, heads, :], op=ALU.add
             )
-            pe_norm = back.tile([P, 1], F32)
-            nc.gpsimd.tensor_scalar(out=pe_norm[:], in0=sum_pe2[:], scalar1=1.0, scalar2=1.0, op0=ALU.mult, op1=ALU.add)
-            sum_k2 = back.tile([P, HEADS], F32)
-            sum_v2 = back.tile([P, HEADS], F32)
-            for half in range(2):
-                heads = slice(HALF_HEADS * half, HALF_HEADS * (half + 1))
-                y = back.tile([P, HALF_HEADS, HEAD_ROWS], F32)
-                y_flat = y[:].rearrange("p h f -> p (h f)")
-                for n in range(HALF_BANKS):
-                    c = HALF_BANKS * half + n
-                    cols = slice(BANK * c, BANK * (c + 1))
-                    y_ps = acc_psum.tile([P, BANK], F32, tag="acc")
-                    nc.tensor.matmul_mx(
-                        out=y_ps[:],
-                        lhsT=sp_codes[:, i, :].bitcast(FP8X4),
-                        lhsT_scale=sp_scales[:, i, :],
-                        rhs=wb_codes[:, cols].bitcast(FP8X4),
-                        rhs_scale=wb_scales[:, cols],
-                        start=True,
-                        stop=True,
-                    )
-                    nc.vector.scalar_tensor_tensor(
-                        out=y_flat[:, BANK * n : BANK * (n + 1)],
-                        in0=w0_all[:, 1 + BANK * c : 1 + BANK * (c + 1)],
-                        scalar=time_t[:, i : i + 1],
-                        in1=y_ps[:],
-                        op0=ALU.mult,
-                        op1=ALU.add,
-                    )
-                nc.gpsimd.tensor_tensor(
-                    out=k_out[:, heads, 1 : 1 + NOPE], in0=y[:, :, 0:NOPE], in1=bias_k[:, heads, :], op=ALU.add
-                )
-                nc.vector.tensor_tensor(out=v_out[:, heads, 1:], in0=y[:, :, NOPE:], in1=bias_v_halves[half][:].rearrange("p (h f) -> p h f", f=V_DIM), op=ALU.add)
-                for h in range(HALF_HEADS * half, HALF_HEADS * (half + 1)):
-                    nc.scalar.activation(
-                        out=junk_head[:, h % 4, :], in_=v_out[:, h, 1:], func=ACT.Square, accum_out=sum_v2[:, h : h + 1]
-                    )
+            nc.vector.tensor_tensor(
+                out=v_out[:, :, 1:], in0=y[:, :, NOPE:], in1=bias_v[:].rearrange("p (h f) -> p h f", f=V_DIM), op=ALU.add
+            )
+            for h in range(HALF_HEADS):
                 nc.scalar.activation(
-                    out=v_out[:, heads, 0], in_=sum_v2[:, heads], func=ACT.Sqrt, bias=one_col[:], scale=1.0
+                    out=junk_head[:, h % 4, :], in_=v_out[:, h, 1:], func=ACT.Square, accum_out=sum_v2[:, h : h + 1]
                 )
-                nc.sync.dma_start(out=v_rows[P * i : P * i + P, heads, :], in_=v_out[:, heads, :])
-                for h in range(HALF_HEADS * half, HALF_HEADS * (half + 1)):
-                    nc.scalar.activation(
-                        out=junk_head[:, h % 4, 0:NOPE],
-                        in_=k_out[:, h, 1 : 1 + NOPE],
-                        func=ACT.Square,
-                        accum_out=sum_k2[:, h : h + 1],
-                    )
+            nc.scalar.activation(out=v_out[:, :, 0], in_=sum_v2[:], func=ACT.Sqrt, bias=one_col[:], scale=1.0)
+            nc.sync.dma_start(out=v_rows[P * i : P * i + P, heads, :], in_=v_out[:])
+            for h in range(HALF_HEADS):
                 nc.scalar.activation(
-                    out=k_out[:, heads, 0], in_=sum_k2[:, heads], func=ACT.Sqrt, bias=pe_norm[:], scale=1.0
+                    out=junk_head[:, h % 4, 0:NOPE],
+                    in_=k_out[:, h, 1 : 1 + NOPE],
+                    func=ACT.Square,
+                    accum_out=sum_k2[:, h : h + 1],
                 )
-                nc.sync.dma_start(out=k_rows[P * i : P * i + P, heads, :], in_=k_out[:, heads, :])
+            nc.scalar.activation(
+                out=k_out[:, :, 0], in_=sum_k2[:], func=ACT.Sqrt, bias=pe_norm[:, i : i + 1], scale=1.0
+            )
+            nc.sync.dma_start(out=k_rows[P * i : P * i + P, heads, :], in_=k_out[:])
 
+        for c in range(HALF_BANKS):
+            prepare_wb(c)
+        bias_v_first = spread_rows(BV_ROW0, HALF_HEADS, pe_psum, "pe")
         for i in range(TOKEN_TILES):
-            second_stage(i)
+            second_stage(i, 0, bias_v_first)
+            if i < HALF_BANKS:
+                prepare_wb(HALF_BANKS + i)
+        bias_v_second = spread_rows(BV_ROW0 + HALF_HEADS, HALF_HEADS, turn_psum, "turned")
+        for i in range(TOKEN_TILES):
+            second_stage(i, 1, bias_v_second)

@@ -319,12 +319,7 @@ def tile_lorentzmla_pa_kernel(
         v_rows = out_1.rearrange("b s h c -> (b s) h c")
         junk_head = keep.tile([P, 4, V_DIM], BF16)
         sum_pe2 = keep.tile([P, TOKEN_TILES], F32)
-        for i in range(TOKEN_TILES):
-            nc.scalar.activation(
-                out=junk_head[:, i, :], in_=k_pe[:, i, :], func=ACT.Square, accum_out=sum_pe2[:, i : i + 1]
-            )
         pe_norm = keep.tile([P, TOKEN_TILES], F32)
-        nc.gpsimd.tensor_scalar(out=pe_norm[:], in0=sum_pe2[:], scalar1=1.0, scalar2=1.0, op0=ALU.mult, op1=ALU.add)
 
         def second_stage(i, half, bias_v):
             heads = slice(HALF_HEADS * half, HALF_HEADS * (half + 1))
@@ -375,6 +370,18 @@ def tile_lorentzmla_pa_kernel(
                 )
             nc.scalar.activation(out=v_out[:, :, 0], in_=sum_v2[:], func=ACT.Sqrt, bias=one_col[:], scale=1.0)
             nc.sync.dma_start(out=v_rows[P * i : P * i + P, heads, :], in_=v_out[:])
+            if half == 0:
+                nc.scalar.activation(
+                    out=junk_head[:, 0, :], in_=k_pe[:, i, :], func=ACT.Square, accum_out=sum_pe2[:, i : i + 1]
+                )
+                nc.gpsimd.tensor_scalar(
+                    out=pe_norm[:, i : i + 1],
+                    in0=sum_pe2[:, i : i + 1],
+                    scalar1=1.0,
+                    scalar2=1.0,
+                    op0=ALU.mult,
+                    op1=ALU.add,
+                )
             for h in range(HALF_HEADS):
                 nc.scalar.activation(
                     out=junk_head[:, h % 4, 0:NOPE],

@@ -187,6 +187,38 @@ def tile_lorentzmla_pa_kernel(
                 in_=grouped[:].rearrange("p g r u -> p (g r u)").bitcast(BF16),
             )
 
+        wb_words = wb_sb[:].bitcast(F32)
+        HALF_HEADS = HEADS // 2
+        HALF_BANKS = B_CHUNKS // 2
+
+        def spread_w0(row_tiles):
+            w0_ps = turn_psum.tile([P, BANK], BF16, tag="turned")
+            for m, n in enumerate(row_tiles):
+                nc.tensor.matmul(
+                    out=w0_ps[:, P * m : P * m + P],
+                    lhsT=wb_sb[:, n, KV_RANK:RUN].to_broadcast([P, P]),
+                    rhs=ident_bf[:],
+                    start=True,
+                    stop=True,
+                )
+            return w0_ps
+
+        def prepare_wb(c):
+            cols = slice(BANK * c, BANK * (c + 1))
+            grouped = regroup([wb_words[:, 4 * c + m, 0:WORDS] for m in range(4)])
+            nc.vector.quantize_mx(
+                out=wb_codes[:, cols].bitcast(FP8X4),
+                scales=wb_scales[:, cols],
+                in_=grouped[:].rearrange("p m r u -> p (m r u)").bitcast(BF16),
+            )
+            w0_ps = spread_w0(range(4 * c, 4 * c + 4))
+            width = min(BANK, B_OUT - 1 - BANK * c)
+            nc.scalar.copy(out=w0_all[:, 2 + BANK * c : 2 + BANK * c + width], in_=w0_ps[:, 0:width])
+
+        def prepare_wrap():
+            wrap_ps = spread_w0([B_TILES - 1])
+            nc.scalar.copy(out=w0_all[:, 1:2], in_=wrap_ps[:, P - 1 : P])
+
         kv_all = front.tile([P, TOKEN_TILES, KV_RANK], F32)
         pe_all = front.tile([P, TOKEN_TILES, ROPE], F32)
         gained = front.tile([P, TOKEN_TILES, KV_RANK], F32)
@@ -226,6 +258,8 @@ def tile_lorentzmla_pa_kernel(
             op=ALU.add,
         )
 
+        prepare_wb(0)
+        prepare_wrap()
         rms = front.tile([P, TOKEN_TILES], F32)
         nc.scalar.activation(out=rms[:], in_=sum_kv2[:], func=ACT.Sqrt, bias=eps_col[:], scale=1.0 / KV_RANK)
         inv_rms = front.tile([P, TOKEN_TILES], F32)
@@ -235,12 +269,14 @@ def tile_lorentzmla_pa_kernel(
             nc.vector.tensor_scalar(
                 out=sp_bf[:, i, :], in0=gained[:, i, :], scalar1=inv_rms[:, i : i + 1], scalar2=None, op0=ALU.mult
             )
+        prepare_wb(1)
         sum_sp2 = front.tile([P, TOKEN_TILES], F32)
         nc.vector.tensor_tensor(out=sum_sp2[:], in0=sum_gained2[:], in1=inv_rms[:], op=ALU.mult)
         nc.vector.tensor_tensor(out=sum_sp2[:], in0=sum_sp2[:], in1=inv_rms[:], op=ALU.mult)
         nc.scalar.activation(out=time_t[:], in_=sum_sp2[:], func=ACT.Sqrt, bias=one_col[:], scale=1.0)
 
         sp_grouped = front.tile([P, TOKEN_TILES, P, 4], BF16, align_bytes=64)
+        between_pairs = ((2,), (3,))
         for pair in range(TOKEN_TILES // 2):
             sp_turned = turn_psum.tile([P, 2, 4, P], BF16, tag="turned")
             for i2 in range(2):
@@ -251,12 +287,15 @@ def tile_lorentzmla_pa_kernel(
             nc.vector.tensor_copy(
                 out=sp_grouped[:, 2 * pair : 2 * pair + 2], in_=sp_turned[:].rearrange("p i t r -> p i r t")
             )
+            for c in between_pairs[pair]:
+                prepare_wb(c)
         nc.vector.quantize_mx(
             out=sp_codes[:].rearrange("p i r -> p (i r)").bitcast(FP8X4),
             scales=sp_scales[:].rearrange("p i r -> p (i r)"),
             in_=sp_grouped[:].rearrange("p i r t -> p (i r t)"),
         )
 
+        prepare_wb(4)
         pe_pairs = pe_all[:].rearrange("p i (j two) -> p (i j) two", two=2)
         even = pe_pairs[:, :, 0].rearrange("p (b hj) -> p b hj", b=2)
         odd = pe_pairs[:, :, 1].rearrange("p (b hj) -> p b hj", b=2)
@@ -283,37 +322,6 @@ def tile_lorentzmla_pa_kernel(
             in1=odd_cos[:].rearrange("p b hj -> p (b hj)"),
             op=ALU.add,
         )
-
-        wb_words = wb_sb[:].bitcast(F32)
-        HALF_HEADS = HEADS // 2
-        HALF_BANKS = B_CHUNKS // 2
-
-        def spread_w0(row_tiles):
-            w0_ps = turn_psum.tile([P, BANK], BF16, tag="turned")
-            for m, n in enumerate(row_tiles):
-                nc.tensor.matmul(
-                    out=w0_ps[:, P * m : P * m + P],
-                    lhsT=wb_sb[:, n, KV_RANK:RUN].to_broadcast([P, P]),
-                    rhs=ident_bf[:],
-                    start=True,
-                    stop=True,
-                )
-            return w0_ps
-
-        def prepare_wb(c):
-            cols = slice(BANK * c, BANK * (c + 1))
-            grouped = regroup([wb_words[:, 4 * c + m, 0:WORDS] for m in range(4)])
-            nc.vector.quantize_mx(
-                out=wb_codes[:, cols].bitcast(FP8X4),
-                scales=wb_scales[:, cols],
-                in_=grouped[:].rearrange("p m r u -> p (m r u)").bitcast(BF16),
-            )
-            w0_ps = spread_w0(range(4 * c, 4 * c + 4))
-            width = min(BANK, B_OUT - 1 - BANK * c)
-            nc.scalar.copy(out=w0_all[:, 2 + BANK * c : 2 + BANK * c + width], in_=w0_ps[:, 0:width])
-
-        wrap_ps = spread_w0([B_TILES - 1])
-        nc.scalar.copy(out=w0_all[:, 1:2], in_=wrap_ps[:, P - 1 : P])
 
         k_rows = out_0.rearrange("b s h c -> (b s) h c")
         v_rows = out_1.rearrange("b s h c -> (b s) h c")
@@ -394,13 +402,12 @@ def tile_lorentzmla_pa_kernel(
             )
             nc.sync.dma_start(out=k_rows[P * i : P * i + P, heads, :], in_=k_out[:])
 
-        for c in range(HALF_BANKS):
-            prepare_wb(c)
+        in_first_round = ((5,), (), (), ())
         bias_v_first = spread_rows(BV_ROW0, HALF_HEADS, pe_psum, "pe")
         for i in range(TOKEN_TILES):
             second_stage(i, 0, bias_v_first)
-            if i < HALF_BANKS:
-                prepare_wb(HALF_BANKS + i)
+            for c in in_first_round[i]:
+                prepare_wb(c)
         bias_v_second = spread_rows(BV_ROW0 + HALF_HEADS, HALF_HEADS, turn_psum, "turned")
         for i in range(TOKEN_TILES):
             second_stage(i, 1, bias_v_second)

@@ -329,43 +329,49 @@ def tile_lorentzmla_pa_kernel(
         sum_pe2 = keep.tile([P, TOKEN_TILES], F32)
         pe_norm = keep.tile([P, TOKEN_TILES], F32)
 
-        def second_stage(i, half, bias_v):
-            heads = slice(HALF_HEADS * half, HALF_HEADS * (half + 1))
-            k_out = outs.tile([P, HALF_HEADS, 1 + NOPE + ROPE], F32)
-            v_out = outs.tile([P, HALF_HEADS, 1 + V_DIM], F32)
-            sum_k2 = outs.tile([P, HALF_HEADS], F32)
-            sum_v2 = outs.tile([P, HALF_HEADS], F32)
-            nc.gpsimd.tensor_scalar(
-                out=k_out[:, :, 1 + NOPE :],
-                in0=k_pe[:, i, :].unsqueeze(1).to_broadcast([P, HALF_HEADS, ROPE]),
-                scalar1=1.0,
-                scalar2=0.0,
-                op0=ALU.mult,
-                op1=ALU.add,
-            )
-            y = back.tile([P, HALF_HEADS, HEAD_ROWS], F32)
-            y_flat = y[:].rearrange("p h f -> p (h f)")
-            for n in range(HALF_BANKS):
-                c = HALF_BANKS * half + n
-                cols = slice(BANK * c, BANK * (c + 1))
-                y_ps = acc_psum.tile([P, BANK], F32, tag="acc")
-                nc.tensor.matmul_mx(
-                    out=y_ps[:],
-                    lhsT=sp_codes[:, i, :].bitcast(FP8X4),
-                    lhsT_scale=sp_scales[:, i, :],
-                    rhs=wb_codes[:, cols].bitcast(FP8X4),
-                    rhs_scale=wb_scales[:, cols],
-                    start=True,
-                    stop=True,
-                )
-                nc.vector.scalar_tensor_tensor(
-                    out=y_flat[:, BANK * n : BANK * (n + 1)],
-                    in0=w0_all[:, 1 + BANK * c : 1 + BANK * (c + 1)],
-                    scalar=time_t[:, i : i + 1],
-                    in1=y_ps[:],
+        tiles_of = {}
+
+        def multiply(i, half, n):
+            if n == 0:
+                k_out = outs.tile([P, HALF_HEADS, 1 + NOPE + ROPE], F32)
+                v_out = outs.tile([P, HALF_HEADS, 1 + V_DIM], F32)
+                y = back.tile([P, HALF_HEADS, HEAD_ROWS], F32)
+                tiles_of[(i, half)] = (k_out, v_out, y)
+                nc.gpsimd.tensor_scalar(
+                    out=k_out[:, :, 1 + NOPE :],
+                    in0=k_pe[:, i, :].unsqueeze(1).to_broadcast([P, HALF_HEADS, ROPE]),
+                    scalar1=1.0,
+                    scalar2=0.0,
                     op0=ALU.mult,
                     op1=ALU.add,
                 )
+            y_flat = tiles_of[(i, half)][2][:].rearrange("p h f -> p (h f)")
+            c = HALF_BANKS * half + n
+            cols = slice(BANK * c, BANK * (c + 1))
+            y_ps = acc_psum.tile([P, BANK], F32, tag="acc")
+            nc.tensor.matmul_mx(
+                out=y_ps[:],
+                lhsT=sp_codes[:, i, :].bitcast(FP8X4),
+                lhsT_scale=sp_scales[:, i, :],
+                rhs=wb_codes[:, cols].bitcast(FP8X4),
+                rhs_scale=wb_scales[:, cols],
+                start=True,
+                stop=True,
+            )
+            nc.vector.scalar_tensor_tensor(
+                out=y_flat[:, BANK * n : BANK * (n + 1)],
+                in0=w0_all[:, 1 + BANK * c : 1 + BANK * (c + 1)],
+                scalar=time_t[:, i : i + 1],
+                in1=y_ps[:],
+                op0=ALU.mult,
+                op1=ALU.add,
+            )
+
+        def finish(i, half, bias_v):
+            heads = slice(HALF_HEADS * half, HALF_HEADS * (half + 1))
+            k_out, v_out, y = tiles_of[(i, half)]
+            sum_k2 = outs.tile([P, HALF_HEADS], F32)
+            sum_v2 = outs.tile([P, HALF_HEADS], F32)
             nc.gpsimd.tensor_tensor(
                 out=k_out[:, :, 1 : 1 + NOPE], in0=y[:, :, 0:NOPE], in1=bias_k[:, heads, :], op=ALU.add
             )
@@ -402,12 +408,17 @@ def tile_lorentzmla_pa_kernel(
             )
             nc.sync.dma_start(out=k_rows[P * i : P * i + P, heads, :], in_=k_out[:])
 
-        in_first_round = ((5,), (), (), ())
-        bias_v_first = spread_rows(BV_ROW0, HALF_HEADS, pe_psum, "pe")
-        for i in range(TOKEN_TILES):
-            second_stage(i, 0, bias_v_first)
-            for c in in_first_round[i]:
-                prepare_wb(c)
-        bias_v_second = spread_rows(BV_ROW0 + HALF_HEADS, HALF_HEADS, turn_psum, "turned")
-        for i in range(TOKEN_TILES):
-            second_stage(i, 1, bias_v_second)
+        rounds = [(i, half) for half in range(2) for i in range(TOKEN_TILES)]
+        bias_v_of = {0: spread_rows(BV_ROW0, HALF_HEADS, pe_psum, "pe")}
+        with tc.manual_schedule(engines={mybir.EngineType.DVE}):
+            multiply(rounds[0][0], rounds[0][1], 0)
+            for r, (i, half) in enumerate(rounds):
+                for n in range(1, HALF_BANKS):
+                    multiply(i, half, n)
+                if r + 1 < len(rounds):
+                    multiply(rounds[r + 1][0], rounds[r + 1][1], 0)
+                if half not in bias_v_of:
+                    bias_v_of[half] = spread_rows(BV_ROW0 + HALF_HEADS * half, HALF_HEADS, turn_psum, "turned")
+                finish(i, half, bias_v_of[half])
+                if r == 0:
+                    prepare_wb(B_CHUNKS - 1)

from contextlib import ExitStack

import concourse.mybir as mybir
from concourse.masks import make_identity

F32 = mybir.dt.float32
BF16 = mybir.dt.bfloat16
U32 = mybir.dt.uint32
U8 = mybir.dt.uint8
FP8X4 = mybir.dt.float8_e4m3fn_x4
ALU = mybir.AluOpType
ACT = mybir.ActivationFunctionType

P = 128
K_PASS = 512
WORDS = K_PASS // 2
BANK = 512

TOKENS = 512
TOKEN_TILES = TOKENS // P
DIM = 2048
PASSES_A = DIM // K_PASS
KV_RANK = 512
ROPE = 128
A_OUT = KV_RANK + ROPE
A_TILES = A_OUT // P
HEADS = 16
NOPE = 64
V_DIM = 128
HEAD_ROWS = NOPE + V_DIM
B_OUT = HEADS * HEAD_ROWS
B_TILES = B_OUT // P
B_CHUNKS = B_OUT // BANK
ROW_SLOT = 528
EPS = 1e-6

FLOPS = 2 * TOKENS * DIM * A_OUT + 2 * TOKENS * KV_RANK * B_OUT


def tile_lorentzmla_pa_kernel(
    tc, x, freqs_cos, freqs_sin, wkv_a_w, wkv_a_b, kv_norm_w, wkv_b_w, wkv_b_b, out_0, out_1
):
    nc = tc.nc
    with ExitStack() as ctx:
        keep = ctx.enter_context(tc.tile_pool(name="keep", bufs=1))
        front = ctx.enter_context(tc.tile_pool(name="front", bufs=1))
        stage = ctx.enter_context(tc.tile_pool(name="stage", bufs=3))
        back = ctx.enter_context(tc.tile_pool(name="back", bufs=2))
        outs = ctx.enter_context(tc.tile_pool(name="outs", bufs=4))
        turn_psum = ctx.enter_context(tc.psum_pool(name="turn_psum", bufs=4))
        acc_psum = ctx.enter_context(tc.psum_pool(name="acc_psum", bufs=3))
        pe_psum = ctx.enter_context(tc.psum_pool(name="pe_psum", bufs=1))

        wa_codes = keep.tile([P, PASSES_A, A_OUT], U32, align_bytes=64)
        wa_scales = keep.tile([P, PASSES_A, A_OUT], U8, align_bytes=64)
        x_codes = keep.tile([P, TOKEN_TILES, PASSES_A * P], U32, align_bytes=64)
        x_scales = keep.tile([P, TOKEN_TILES, PASSES_A * P], U8, align_bytes=64)
        sp_codes = keep.tile([P, TOKEN_TILES, P], U32, align_bytes=64)
        sp_scales = keep.tile([P, TOKEN_TILES, P], U8, align_bytes=64)
        wb_codes = keep.tile([P, B_OUT], U32, align_bytes=64)
        wb_scales = keep.tile([P, B_OUT], U8, align_bytes=64)
        w0_all = keep.tile([P, 2 + B_OUT], BF16)
        bias_k = keep.tile([P, HEADS, NOPE], BF16)
        time_t = keep.tile([P, TOKEN_TILES], F32)
        k_pe = keep.tile([P, TOKEN_TILES, ROPE], F32)

        ident_f32 = keep.tile([P, P], F32)
        make_identity(nc, ident_f32[:])
        ident_bf = keep.tile([P, P], BF16)
        make_identity(nc, ident_bf[:])
        one_col = keep.tile([P, 1], F32)
        nc.vector.memset(one_col[:], 1.0)
        eps_col = keep.tile([P, 1], F32)
        nc.vector.memset(eps_col[:], EPS)
        warm = keep.tile([P, 1], F32)
        nc.scalar.activation(out=warm[:], in_=one_col[:], func=ACT.Sqrt)

        def regroup(sources):
            grouped = stage.tile([P, 4, P, 2], F32, align_bytes=64)
            for half in range(2):
                turned = turn_psum.tile([P, 2, 2, P], F32, tag="turned")
                for s in range(2):
                    for u in range(2):
                        nc.tensor.transpose(
                            turned[:, s, u, :], sources[2 * half + s][:, P * u : P * u + P], ident_f32[:]
                        )
                nc.scalar.copy(
                    out=grouped[:, 2 * half : 2 * half + 2], in_=turned[:].rearrange("p s u r -> p s r u")
                )
            return grouped

        A_ROW0, G_ROW0, BV_ROW0, BK_ROW0 = 0, 32, 64, 96
        vec_rows = keep.tile([P, P], BF16)
        nc.vector.memset(vec_rows[:], 0.0)
        nc.sync.dma_start(
            out=vec_rows[A_ROW0 : A_ROW0 + A_TILES, :], in_=wkv_a_b.rearrange("(r c) -> r c", c=P)
        )
        nc.sync.dma_start(
            out=vec_rows[G_ROW0 : G_ROW0 + KV_RANK // P, :], in_=kv_norm_w.rearrange("(r c) -> r c", c=P)
        )
        nc.sync.dma_start(
            out=vec_rows[BV_ROW0 : BV_ROW0 + HEADS, :],
            in_=wkv_b_b.rearrange("(h f) -> h f", f=HEAD_ROWS)[:, NOPE:HEAD_ROWS],
        )
        nc.sync.dma_start(
            out=vec_rows[BK_ROW0 : BK_ROW0 + HEADS // 2, :].rearrange("r (two f) -> r two f", two=2),
            in_=wkv_b_b.rearrange("(r two f) -> r two f", two=2, f=HEAD_ROWS)[:, :, 0:NOPE],
        )
        wa_sb = front.tile([P, A_TILES, DIM], BF16)
        kv_rows = wkv_a_w[0:KV_RANK, :].rearrange("(u q e) k -> u e q k", u=2, e=2)
        for j in range(KV_RANK // P):
            nc.sync.dma_start(out=wa_sb[:, j, :], in_=kv_rows[j // 2, j % 2])
        nc.sync.dma_start(out=wa_sb[:, KV_RANK // P, :], in_=wkv_a_w[KV_RANK:A_OUT, :])
        x_sb = front.tile([P, TOKEN_TILES, DIM], BF16)
        x_rows = x.rearrange("b s k -> (b s) k")
        for i in range(TOKEN_TILES):
            nc.sync.dma_start(out=x_sb[:, i, :], in_=x_rows[P * i : P * i + P, :])
        cos_sb = front.tile([P, 2, ROPE // 2], BF16)
        nc.sync.dma_start(out=cos_sb[:], in_=freqs_cos.rearrange("(h p) j -> p h j", p=P))
        sin_sb = front.tile([P, 2, ROPE // 2], BF16)
        nc.sync.dma_start(out=sin_sb[:], in_=freqs_sin.rearrange("(h p) j -> p h j", p=P))
        wb_sb = front.tile([P, B_TILES, ROW_SLOT], BF16)
        wb_flat = wkv_b_w.rearrange("r c -> (r c)")
        RUN = KV_RANK + 1
        FULL_TILES = B_TILES - 1
        wb_runs = wb_flat[1 : 1 + FULL_TILES * P * RUN].rearrange("(n p c) -> p n c", p=P, c=RUN)
        tail0 = 1 + FULL_TILES * P * RUN
        nc.sync.dma_start(
            out=wb_sb[0 : P - 1, FULL_TILES, 0:RUN],
            in_=wb_flat[tail0 : tail0 + (P - 1) * RUN].rearrange("(p c) -> p c", c=RUN),
        )
        nc.sync.dma_start(
            out=wb_sb[P - 1 : P, FULL_TILES, 0:KV_RANK],
            in_=wb_flat[tail0 + (P - 1) * RUN : tail0 + (P - 1) * RUN + KV_RANK].rearrange("(p c) -> p c", p=1),
        )
        nc.sync.dma_start(
            out=wb_sb[P - 1 : P, FULL_TILES, KV_RANK:RUN], in_=wb_flat[0:1].rearrange("(p c) -> p c", p=1)
        )
        for c in range(B_CHUNKS):
            last = min(4 * c + 4, FULL_TILES)
            nc.sync.dma_start(out=wb_sb[:, 4 * c : last, 0:RUN], in_=wb_runs[:, 4 * c : last, :])

        def spread_rows(first_row, n_rows, pool, tag):
            spread = pool.tile([P, 2 * BANK], BF16, tag=tag)
            for r in range(n_rows):
                nc.tensor.matmul(
                    out=spread[:, P * r : P * r + P],
                    lhsT=ident_bf[:, first_row + r : first_row + r + 1].to_broadcast([P, P]),
                    rhs=vec_rows[:],
                    start=True,
                    stop=True,
                )
            return spread

        bias_a = front.tile([P, A_OUT], BF16)
        spread_a = spread_rows(A_ROW0, A_TILES, turn_psum, "turned")
        nc.vector.tensor_copy(
            out=bias_a[:, 0:KV_RANK].rearrange("p (u e q) -> p u e q", u=2, e=2),
            in_=spread_a[:, 0:KV_RANK].rearrange("p (u q e) -> p u e q", u=2, e=2),
        )
        nc.vector.tensor_copy(out=bias_a[:, KV_RANK:A_OUT], in_=spread_a[:, KV_RANK:A_OUT])
        gain = front.tile([P, KV_RANK], BF16)
        spread_g = spread_rows(G_ROW0, KV_RANK // P, turn_psum, "turned")
        nc.vector.tensor_copy(
            out=gain[:].rearrange("p (u e q) -> p u e q", u=2, e=2),
            in_=spread_g[:, 0:KV_RANK].rearrange("p (u q e) -> p u e q", u=2, e=2),
        )

        spread_k = spread_rows(BK_ROW0, HEADS // 2, turn_psum, "turned")
        nc.vector.tensor_copy(out=bias_k[:].rearrange("p h f -> p (h f)"), in_=spread_k[:])

        wa_words = wa_sb[:].bitcast(F32)
        for j in range(A_TILES):
            grouped = regroup([wa_words[:, j, WORDS * g : WORDS * (g + 1)] for g in range(PASSES_A)])
            for g in range(PASSES_A):
                nc.vector.quantize_mx(
                    out=wa_codes[:, g, P * j : P * j + P].bitcast(FP8X4),
                    scales=wa_scales[:, g, P * j : P * j + P],
                    in_=grouped[:, g].rearrange("p r u -> p (r u)").bitcast(BF16),
                )
        x_words = x_sb[:].bitcast(F32)
        for i in range(TOKEN_TILES):
            grouped = regroup([x_words[:, i, WORDS * g : WORDS * (g + 1)] for g in range(PASSES_A)])
            nc.vector.quantize_mx(
                out=x_codes[:, i, :].bitcast(FP8X4),
                scales=x_scales[:, i, :],
                in_=grouped[:].rearrange("p g r u -> p (g r u)").bitcast(BF16),
            )

        wb_words = wb_sb[:].bitcast(F32)
        HALF_HEADS = HEADS // 2
        HALF_BANKS = B_CHUNKS // 2

        def spread_w0(row_tiles):
            w0_ps = turn_psum.tile([P, BANK], BF16, tag="turned")
            for m, n in enumerate(row_tiles):
                nc.tensor.matmul(
                    out=w0_ps[:, P * m : P * m + P],
                    lhsT=wb_sb[:, n, KV_RANK:RUN].to_broadcast([P, P]),
                    rhs=ident_bf[:],
                    start=True,
                    stop=True,
                )
            return w0_ps

        def prepare_wb(c):
            cols = slice(BANK * c, BANK * (c + 1))
            grouped = regroup([wb_words[:, 4 * c + m, 0:WORDS] for m in range(4)])
            nc.vector.quantize_mx(
                out=wb_codes[:, cols].bitcast(FP8X4),
                scales=wb_scales[:, cols],
                in_=grouped[:].rearrange("p m r u -> p (m r u)").bitcast(BF16),
            )
            w0_ps = spread_w0(range(4 * c, 4 * c + 4))
            width = min(BANK, B_OUT - 1 - BANK * c)
            nc.scalar.copy(out=w0_all[:, 2 + BANK * c : 2 + BANK * c + width], in_=w0_ps[:, 0:width])

        def prepare_wrap():
            wrap_ps = spread_w0([B_TILES - 1])
            nc.scalar.copy(out=w0_all[:, 1:2], in_=wrap_ps[:, P - 1 : P])

        kv_all = front.tile([P, TOKEN_TILES, KV_RANK], F32)
        pe_all = front.tile([P, TOKEN_TILES, ROPE], F32)
        gained = front.tile([P, TOKEN_TILES, KV_RANK], F32)
        junk_kv = front.tile([P, 2, KV_RANK], BF16)
        junk_gained = front.tile([P, 2, KV_RANK], BF16)
        sum_kv2 = front.tile([P, TOKEN_TILES], F32)
        sum_gained2 = front.tile([P, TOKEN_TILES], F32)
        pe_ps = pe_psum.tile([P, TOKEN_TILES, ROPE], F32, tag="pe")
        for i in range(TOKEN_TILES):
            kv_ps = acc_psum.tile([P, BANK], F32, tag="acc")
            for out_ps, cols in ((kv_ps[:], slice(0, KV_RANK)), (pe_ps[:, i, :], slice(KV_RANK, A_OUT))):
                for g in range(PASSES_A):
                    nc.tensor.matmul_mx(
                        out=out_ps,
                        lhsT=x_codes[:, i, P * g : P * g + P].bitcast(FP8X4),
                        lhsT_scale=x_scales[:, i, P * g : P * g + P],
                        rhs=wa_codes[:, g, cols].bitcast(FP8X4),
                        rhs_scale=wa_scales[:, g, cols],
                        start=(g == 0),
                        stop=(g == PASSES_A - 1),
                    )
            nc.vector.tensor_tensor(out=kv_all[:, i, :], in0=kv_ps[:], in1=bias_a[:, 0:KV_RANK], op=ALU.add)
            nc.scalar.activation(
                out=junk_kv[:, i % 2, :], in_=kv_all[:, i, :], func=ACT.Square, accum_out=sum_kv2[:, i : i + 1]
            )
            nc.vector.tensor_tensor(out=gained[:, i, :], in0=kv_all[:, i, :], in1=gain[:], op=ALU.mult)
            nc.scalar.activation(
                out=junk_gained[:, i % 2, :],
                in_=gained[:, i, :],
                func=ACT.Square,
                accum_out=sum_gained2[:, i : i + 1],
            )
        nc.vector.tensor_tensor(
            out=pe_all[:],
            in0=pe_ps[:],
            in1=bias_a[:, KV_RANK:A_OUT].unsqueeze(1).to_broadcast([P, TOKEN_TILES, ROPE]),
            op=ALU.add,
        )

        prepare_wb(0)
        prepare_wrap()
        rms = front.tile([P, TOKEN_TILES], F32)
        nc.scalar.activation(out=rms[:], in_=sum_kv2[:], func=ACT.Sqrt, bias=eps_col[:], scale=1.0 / KV_RANK)
        inv_rms = front.tile([P, TOKEN_TILES], F32)
        nc.vector.reciprocal(out=inv_rms[:], in_=rms[:])
        sp_bf = front.tile([P, TOKEN_TILES, KV_RANK], BF16)
        for i in range(TOKEN_TILES):
            nc.vector.tensor_scalar(
                out=sp_bf[:, i, :], in0=gained[:, i, :], scalar1=inv_rms[:, i : i + 1], scalar2=None, op0=ALU.mult
            )
        prepare_wb(1)
        sum_sp2 = front.tile([P, TOKEN_TILES], F32)
        nc.vector.tensor_tensor(out=sum_sp2[:], in0=sum_gained2[:], in1=inv_rms[:], op=ALU.mult)
        nc.vector.tensor_tensor(out=sum_sp2[:], in0=sum_sp2[:], in1=inv_rms[:], op=ALU.mult)
        nc.scalar.activation(out=time_t[:], in_=sum_sp2[:], func=ACT.Sqrt, bias=one_col[:], scale=1.0)

        sp_grouped = front.tile([P, TOKEN_TILES, P, 4], BF16, align_bytes=64)
        between_pairs = ((2,), (3,))
        for pair in range(TOKEN_TILES // 2):
            sp_turned = turn_psum.tile([P, 2, 4, P], BF16, tag="turned")
            for i2 in range(2):
                for t in range(4):
                    nc.tensor.transpose(
                        sp_turned[:, i2, t, :], sp_bf[:, 2 * pair + i2, P * t : P * t + P], ident_bf[:]
                    )
            nc.vector.tensor_copy(
                out=sp_grouped[:, 2 * pair : 2 * pair + 2], in_=sp_turned[:].rearrange("p i t r -> p i r t")
            )
            for c in between_pairs[pair]:
                prepare_wb(c)
        nc.vector.quantize_mx(
            out=sp_codes[:].rearrange("p i r -> p (i r)").bitcast(FP8X4),
            scales=sp_scales[:].rearrange("p i r -> p (i r)"),
            in_=sp_grouped[:].rearrange("p i r t -> p (i r t)"),
        )

        prepare_wb(4)
        pe_pairs = pe_all[:].rearrange("p i (j two) -> p (i j) two", two=2)
        even = pe_pairs[:, :, 0].rearrange("p (b hj) -> p b hj", b=2)
        odd = pe_pairs[:, :, 1].rearrange("p (b hj) -> p b hj", b=2)
        cos = cos_sb[:].rearrange("p h j -> p (h j)").unsqueeze(1).to_broadcast([P, 2, ROPE])
        sin = sin_sb[:].rearrange("p h j -> p (h j)").unsqueeze(1).to_broadcast([P, 2, ROPE])
        even_cos = front.tile([P, 2, ROPE], F32)
        nc.gpsimd.tensor_tensor(out=even_cos[:], in0=even, in1=cos, op=ALU.mult)
        odd_sin = front.tile([P, 2, ROPE], F32)
        nc.gpsimd.tensor_tensor(out=odd_sin[:], in0=odd, in1=sin, op=ALU.mult)
        even_sin = front.tile([P, 2, ROPE], F32)
        nc.gpsimd.tensor_tensor(out=even_sin[:], in0=even, in1=sin, op=ALU.mult)
        odd_cos = front.tile([P, 2, ROPE], F32)
        nc.gpsimd.tensor_tensor(out=odd_cos[:], in0=odd, in1=cos, op=ALU.mult)
        k_pe_pairs = k_pe[:].rearrange("p i (j two) -> p (i j) two", two=2)
        nc.gpsimd.tensor_tensor(
            out=k_pe_pairs[:, :, 0],
            in0=even_cos[:].rearrange("p b hj -> p (b hj)"),
            in1=odd_sin[:].rearrange("p b hj -> p (b hj)"),
            op=ALU.subtract,
        )
        nc.gpsimd.tensor_tensor(
            out=k_pe_pairs[:, :, 1],
            in0=even_sin[:].rearrange("p b hj -> p (b hj)"),
            in1=odd_cos[:].rearrange("p b hj -> p (b hj)"),
            op=ALU.add,
        )

        k_rows = out_0.rearrange("b s h c -> (b s) h c")
        v_rows = out_1.rearrange("b s h c -> (b s) h c")
        junk_head = keep.tile([P, 4, V_DIM], BF16)
        sum_pe2 = keep.tile([P, TOKEN_TILES], F32)
        pe_norm = keep.tile([P, TOKEN_TILES], F32)

        tiles_of = {}

        def multiply(i, half, n):
            if n == 0:
                k_out = outs.tile([P, HALF_HEADS, 1 + NOPE + ROPE], F32)
                v_out = outs.tile([P, HALF_HEADS, 1 + V_DIM], F32)
                y = back.tile([P, HALF_HEADS, HEAD_ROWS], F32)
                tiles_of[(i, half)] = (k_out, v_out, y)
                nc.gpsimd.tensor_scalar(
                    out=k_out[:, :, 1 + NOPE :],
                    in0=k_pe[:, i, :].unsqueeze(1).to_broadcast([P, HALF_HEADS, ROPE]),
                    scalar1=1.0,
                    scalar2=0.0,
                    op0=ALU.mult,
                    op1=ALU.add,
                )
            y_flat = tiles_of[(i, half)][2][:].rearrange("p h f -> p (h f)")
            c = HALF_BANKS * half + n
            cols = slice(BANK * c, BANK * (c + 1))
            y_ps = acc_psum.tile([P, BANK], F32, tag="acc")
            nc.tensor.matmul_mx(
                out=y_ps[:],
                lhsT=sp_codes[:, i, :].bitcast(FP8X4),
                lhsT_scale=sp_scales[:, i, :],
                rhs=wb_codes[:, cols].bitcast(FP8X4),
                rhs_scale=wb_scales[:, cols],
                start=True,
                stop=True,
            )
            nc.vector.scalar_tensor_tensor(
                out=y_flat[:, BANK * n : BANK * (n + 1)],
                in0=w0_all[:, 1 + BANK * c : 1 + BANK * (c + 1)],
                scalar=time_t[:, i : i + 1],
                in1=y_ps[:],
                op0=ALU.mult,
                op1=ALU.add,
            )

        def finish(i, half, bias_v):
            heads = slice(HALF_HEADS * half, HALF_HEADS * (half + 1))
            k_out, v_out, y = tiles_of[(i, half)]
            sum_k2 = outs.tile([P, HALF_HEADS], F32)
            sum_v2 = outs.tile([P, HALF_HEADS], F32)
            nc.gpsimd.tensor_tensor(
                out=k_out[:, :, 1 : 1 + NOPE], in0=y[:, :, 0:NOPE], in1=bias_k[:, heads, :], op=ALU.add
            )
            nc.vector.tensor_tensor(
                out=v_out[:, :, 1:], in0=y[:, :, NOPE:], in1=bias_v[:].rearrange("p (h f) -> p h f", f=V_DIM), op=ALU.add
            )
            for h in range(HALF_HEADS):
                nc.scalar.activation(
                    out=junk_head[:, h % 4, :], in_=v_out[:, h, 1:], func=ACT.Square, accum_out=sum_v2[:, h : h + 1]
                )
            nc.scalar.activation(out=v_out[:, :, 0], in_=sum_v2[:], func=ACT.Sqrt, bias=one_col[:], scale=1.0)
            nc.sync.dma_start(out=v_rows[P * i : P * i + P, heads, :], in_=v_out[:])
            if half == 0:
                nc.scalar.activation(
                    out=junk_head[:, 0, :], in_=k_pe[:, i, :], func=ACT.Square, accum_out=sum_pe2[:, i : i + 1]
                )
                nc.gpsimd.tensor_scalar(
                    out=pe_norm[:, i : i + 1],
                    in0=sum_pe2[:, i : i + 1],
                    scalar1=1.0,
                    scalar2=1.0,
                    op0=ALU.mult,
                    op1=ALU.add,
                )
            for h in range(HALF_HEADS):
                nc.scalar.activation(
                    out=junk_head[:, h % 4, 0:NOPE],
                    in_=k_out[:, h, 1 : 1 + NOPE],
                    func=ACT.Square,
                    accum_out=sum_k2[:, h : h + 1],
                )
            nc.scalar.activation(
                out=k_out[:, :, 0], in_=sum_k2[:], func=ACT.Sqrt, bias=pe_norm[:, i : i + 1], scale=1.0
            )
            nc.sync.dma_start(out=k_rows[P * i : P * i + P, heads, :], in_=k_out[:])

        rounds = [(i, half) for half in range(2) for i in range(TOKEN_TILES)]
        bias_v_of = {0: spread_rows(BV_ROW0, HALF_HEADS, pe_psum, "pe")}
        with tc.manual_schedule(engines={mybir.EngineType.DVE}):
            multiply(rounds[0][0], rounds[0][1], 0)
            for r, (i, half) in enumerate(rounds):
                for n in range(1, HALF_BANKS):
                    multiply(i, half, n)
                if r + 1 < len(rounds):
                    multiply(rounds[r + 1][0], rounds[r + 1][1], 0)
                if half not in bias_v_of:
                    bias_v_of[half] = spread_rows(BV_ROW0 + HALF_HEADS * half, HALF_HEADS, turn_psum, "turned")
                finish(i, half, bias_v_of[half])
                if r == 0:
                    prepare_wb(B_CHUNKS - 1)
